import numpy as np
import ml_dtypes


def mxq(x, axis, fmt="e4m3"):
    dtype, down = {"e4m3": (ml_dtypes.float8_e4m3fn, 7), "e5m2": (ml_dtypes.float8_e5m2, 14)}[fmt]
    v = np.moveaxis(np.asarray(x, np.float32).astype(ml_dtypes.bfloat16).astype(np.float64), axis, -1)
    blocks = v.reshape(v.shape[:-1] + (-1, 32))
    amax = np.abs(blocks).max(-1, keepdims=True)
    byte = np.maximum(np.where(amax > 0, np.frexp(amax)[1] - 1 + 127, 0) - down, 1)
    scale = np.exp2(byte - 127.0)
    codes = (blocks / scale).astype(np.float32).astype(dtype).astype(np.float64)
    return np.moveaxis((codes * scale).reshape(v.shape), -1, axis)


WIDE = False


def mx_kscale(k):
    if not WIDE:
        return np.ones(k)
    levels = np.array([10, -10, 5, -5, 0])
    a = np.random.permutation(np.resize(levels, k // 512 * 4)).reshape(k // 512, 4)
    idx = np.arange(k)
    return np.exp2(a[idx // 512, idx % 128 // 32])


BF16 = ml_dtypes.bfloat16


def bf(x):
    return np.asarray(x, np.float32).astype(BF16)


def f64(x):
    return np.asarray(x).astype(np.float64)


B, P, C, HS, NG = 2, 512, 256, 2048, 8
GMIN, GMAX = -1.0, 1.0
SKIP = 1.0


def silu(v):
    return v / (1.0 + np.exp(-v))


def rbf(v):
    grid = np.linspace(GMIN, GMAX, NG)
    denom = (GMAX - GMIN) / (NG - 1)
    return np.exp(-np.square((v[..., None] - grid) / denom))


def setup_inputs():
    s = mx_kscale(HS * NG)[::NG]
    u = s / s.max()
    r = np.sqrt(np.log(1.0 / u))
    d = (GMAX - GMIN) / (NG - 1)
    m = (GMAX + d * r) * (r > 0)
    return {"h_mix": bf(np.random.standard_normal((B, C, HS)) * 0.9 * (d / (d + 2.0 * r)) + m),
            "x": bf(np.random.standard_normal((B, P, C))),
            "fc2_spline_w": bf(np.random.standard_normal((P, HS * NG)) * 0.7 / np.sqrt(HS) / np.repeat(u, NG)),
            "fc2_base_w": bf(np.random.standard_normal((P, HS)) / np.sqrt(HS) / (1.0 + m)),
            "fc2_base_b": bf(np.random.standard_normal(P) * 0.1)}


def reference(h_mix, x, fc2_spline_w, fc2_base_w, fc2_base_b):
    h = f64(h_mix)
    basis = rbf(h).reshape(B, C, HS * NG)
    out = mxq(basis, 2, "e4m3") @ mxq(f64(fc2_spline_w).T, 0, "e4m3")
    out = out + (mxq(silu(h), 2, "e4m3") @ mxq(f64(fc2_base_w).T, 0, "e4m3")) + f64(fc2_base_b)
    return np.swapaxes(out, 1, 2) + SKIP * f64(x)

@@ -1,0 +1,229 @@
+from contextlib import ExitStack
+
+import concourse.mybir as mybir
+from concourse.masks import make_identity
+
+F32 = mybir.dt.float32
+BF16 = mybir.dt.bfloat16
+I32 = mybir.dt.int32
+U32 = mybir.dt.uint32
+U8 = mybir.dt.uint8
+FP8X4 = mybir.dt.float8_e4m3fn_x4
+ACT = mybir.ActivationFunctionType
+ALU = mybir.AluOpType
+
+P = 128
+PACK = 4
+K_PASS = P * PACK
+WORDS = K_PASS // 2
+
+TOKENS = 512
+TOKEN_TILES = TOKENS // P
+HIDDEN = 2048
+CENTRES = 8
+OUT_TILES = 4
+CHANNELS = 256
+
+CHUNK_PASSES = 4
+CHUNK_K = CHUNK_PASSES * K_PASS
+SPLINE_CHUNKS = HIDDEN * CENTRES // CHUNK_K
+CHUNK_HIDDEN = CHUNK_K // CENTRES
+COPIES = 4
+GROUP_HIDDEN = P // COPIES
+CHUNK_GROUPS = CHUNK_HIDDEN // GROUP_HIDDEN
+PARKED_CHUNKS = 4
+
+INV_D = 3.5
+
+FLOPS = 2 * TOKENS * 512 * (HIDDEN * CENTRES + HIDDEN)
+
+
+def quantise(nc, codes, scales, values):
+    nc.vector.quantize_mx(out=codes.bitcast(FP8X4), scales=scales, in_=values)
+
+
+def tile_kan1_pb_k_kernel(tc, h_mix, x, fc2_spline_w, fc2_base_w, fc2_base_b, out):
+    nc = tc.nc
+    h_rows = h_mix.flatten_outer_dims()
+    x_rows = x.flatten_outer_dims().rearrange("(g r) c -> r g c", r=P)
+    out_rows = out.flatten_outer_dims()
+    out_tiles = out_rows.rearrange("(g r) c -> r g c", r=P)
+
+    with ExitStack() as stack:
+        keep = stack.enter_context(tc.tile_pool(name="keep", bufs=1))
+        w_raw_pool = stack.enter_context(tc.tile_pool(name="w_raw", bufs=3))
+        w_pool = stack.enter_context(tc.tile_pool(name="w", bufs=2))
+        w_mx_pool = stack.enter_context(tc.tile_pool(name="w_mx", bufs=6))
+        h_t_pool = stack.enter_context(tc.tile_pool(name="h_t", bufs=PARKED_CHUNKS))
+        h_rep_pool = stack.enter_context(tc.tile_pool(name="h_rep", bufs=PARKED_CHUNKS))
+        act_pool = stack.enter_context(tc.tile_pool(name="act", bufs=2))
+        act_mx_pool = stack.enter_context(tc.tile_pool(name="act_mx", bufs=3))
+        res_pool = stack.enter_context(tc.tile_pool(name="res", bufs=OUT_TILES))
+        y_pool = stack.enter_context(tc.psum_pool(name="y", bufs=1))
+        turn_pool = stack.enter_context(tc.psum_pool(name="turn", bufs=4))
+
+        ident_bf = keep.tile([P, P], BF16)
+        make_identity(nc, ident_bf[:])
+        ident_f32 = keep.tile([P, P], F32)
+        make_identity(nc, ident_f32[:])
+
+        part_idx = keep.tile([P, 1], I32)
+        nc.gpsimd.iota(part_idx[:], pattern=[[0, 1]], base=0, channel_multiplier=1)
+        part_mod = keep.tile([P, 1], I32)
+        nc.vector.tensor_single_scalar(out=part_mod[:], in_=part_idx[:], scalar=COPIES - 1, op=ALU.bitwise_and)
+        part_mod_f = keep.tile([P, 1], F32)
+        nc.vector.tensor_copy(out=part_mod_f[:], in_=part_mod[:])
+        centre = keep.tile([P, 2], F32)
+        minus_centre = keep.tile([P, 2], F32)
+        for e in range(2):
+            nc.vector.tensor_scalar(
+                out=centre[:, e : e + 1], in0=part_mod_f[:], scalar1=2.0, scalar2=e - 3.5, op0=ALU.mult, op1=ALU.add
+            )
+            nc.vector.tensor_scalar(
+                out=minus_centre[:, e : e + 1], in0=part_mod_f[:], scalar1=-2.0, scalar2=3.5 - e, op0=ALU.mult, op1=ALU.add
+            )
+
+        h_sb = keep.tile([P, TOKEN_TILES, HIDDEN], BF16)
+        for quarter in range(4):
+            cols = slice(quarter * K_PASS, (quarter + 1) * K_PASS)
+            nc.sync.dma_start(out=h_sb[:, :, cols], in_=h_rows[:, cols].rearrange("(t r) j -> r t j", r=P))
+        x_sb = keep.tile([P, 2 * OUT_TILES, CHANNELS], BF16)
+        nc.gpsimd.dma_start(out=x_sb[:], in_=x_rows)
+        bias_rows = keep.tile([P, P], BF16)
+        nc.vector.memset(bias_rows[:], 0.0)
+        nc.gpsimd.dma_start(out=bias_rows[0:OUT_TILES, :], in_=fc2_base_b.rearrange("(m r) -> m r", r=P))
+
+        def replicate_hidden(chunk):
+            h_t_ps = turn_pool.tile([P, 2, TOKENS], BF16, tag="turn")
+            for half in range(2):
+                first = chunk * CHUNK_HIDDEN + half * P
+                for t in range(TOKEN_TILES):
+                    nc.tensor.transpose(
+                        h_t_ps[:, half, t * P : (t + 1) * P], h_sb[:, t, first : first + P], ident_bf[:]
+                    )
+            h_t = h_t_pool.tile([P, 2, TOKENS], BF16)
+            nc.vector.tensor_copy(out=h_t[:], in_=h_t_ps[:])
+            first_row = (chunk % PARKED_CHUNKS) * CHUNK_HIDDEN
+            parked = out_rows[first_row : first_row + CHUNK_HIDDEN, :]
+            nc.sync.dma_start(out=parked.rearrange("(a r) w -> r a w", r=P), in_=h_t[:].bitcast(F32))
+            h_rep = h_rep_pool.tile([P, CHUNK_GROUPS, TOKENS], BF16)
+            for copy in range(COPIES):
+                nc.sync.dma_start(
+                    out=h_rep[copy:P:COPIES, :, :].bitcast(F32),
+                    in_=parked.rearrange("(a r) w -> r a w", r=GROUP_HIDDEN),
+                )
+            return h_rep
+
+        h_reps = [replicate_hidden(chunk) for chunk in range(PARKED_CHUNKS)]
+
+        silu_codes = keep.tile([P, CHUNK_PASSES, TOKENS], U32, align_bytes=64)
+        silu_scales = keep.tile([P, CHUNK_PASSES, TOKENS], U8, align_bytes=64)
+        for g in range(CHUNK_PASSES):
+            silu_bf = act_pool.tile([P, TOKENS, PACK], BF16, align_bytes=64)
+            for half in range(2):
+                h_w_ps = turn_pool.tile([P, 2, 2 * P], F32, tag="turn")
+                for u in range(2):
+                    first = g * WORDS + u * P
+                    for t in range(2):
+                        nc.tensor.transpose(
+                            h_w_ps[:, u, t * P : (t + 1) * P],
+                            h_sb[:, 2 * half + t, :].bitcast(F32)[:, first : first + P],
+                            ident_f32[:],
+                        )
+                nc.scalar.activation(
+                    out=silu_bf[:, half * 2 * P : (half + 1) * 2 * P, :].rearrange("q n (u e) -> q n u e", u=2),
+                    in_=h_w_ps[:].bitcast(BF16).rearrange("q u (n e) -> q n u e", e=2),
+                    func=ACT.Silu,
+                )
+            quantise(nc, silu_codes[:, g, :], silu_scales[:, g, :], silu_bf[:].rearrange("q n t -> q (n t)"))
+
+        bias_ps = turn_pool.tile([P, P], BF16, tag="turn")
+        nc.tensor.transpose(bias_ps[:], bias_rows[:], ident_bf[:])
+        bias_col = keep.tile([P, OUT_TILES], F32)
+        nc.vector.tensor_copy(out=bias_col[:], in_=bias_ps[:, 0:OUT_TILES])
+
+        y_ps = [y_pool.tile([P, TOKENS], F32, name="y_ps%d" % m) for m in range(OUT_TILES)]
+
+        def quantised_weights(w_raw, g):
+            w_bf = w_pool.tile([P, OUT_TILES * P * PACK], BF16, align_bytes=64)
+            w_words = w_bf[:].bitcast(F32).rearrange("q (b m n u) -> q b m n u", b=2, m=2, u=2)
+            for bank in range(2):
+                w_t_ps = turn_pool.tile([P, 2, 2, P], F32, tag="turn")
+                for m in range(2):
+                    for u in range(2):
+                        first = g * WORDS + u * P
+                        nc.tensor.transpose(
+                            w_t_ps[:, m, u, :],
+                            w_raw[:, 2 * bank + m, :].bitcast(F32)[:, first : first + P],
+                            ident_f32[:],
+                        )
+                source = w_t_ps[:].rearrange("q m u n -> q m n u")
+                if bank == 0:
+                    nc.scalar.copy(out=w_words[:, bank], in_=source)
+                else:
+                    nc.vector.tensor_copy(out=w_words[:, bank], in_=source)
+            w_codes = w_mx_pool.tile([P, OUT_TILES * P], U32, align_bytes=64)
+            w_scales = w_mx_pool.tile([P, OUT_TILES * P], U8, align_bytes=64)
+            quantise(nc, w_codes[:], w_scales[:], w_bf[:])
+            return w_codes, w_scales
+
+        def quantised_basis(h_rep, g):
+            h_pair = h_rep[:, 2 * g : 2 * g + 2, :].rearrange("q u n -> q n u")
+            square = act_pool.tile([P, 2, TOKENS * 2], F32)
+            offset = act_pool.tile([P, TOKENS, 2], F32)
+            nc.vector.tensor_scalar(
+                out=offset[:], in0=h_pair, scalar1=INV_D, scalar2=centre[:, 0:1], op0=ALU.mult, op1=ALU.subtract
+            )
+            offset_flat = offset[:].rearrange("q n u -> q (n u)")
+            nc.vector.tensor_tensor(out=square[:, 0, :], in0=offset_flat, in1=offset_flat, op=ALU.mult)
+            nc.scalar.activation(
+                out=square[:, 1, :].rearrange("q (n u) -> q n u", u=2),
+                in_=h_pair,
+                func=ACT.Square,
+                scale=INV_D,
+                bias=minus_centre[:, 1:2],
+            )
+            basis_bf = act_pool.tile([P, TOKENS * 2, 2], BF16, align_bytes=64)
+            nc.scalar.activation(
+                out=basis_bf[:], in_=square[:].rearrange("q e n -> q n e"), func=ACT.Exp, scale=-1.0
+            )
+            codes = act_mx_pool.tile([P, TOKENS], U32, align_bytes=64)
+            scales = act_mx_pool.tile([P, TOKENS], U8, align_bytes=64)
+            quantise(nc, codes[:], scales[:], basis_bf[:].rearrange("q n e -> q (n e)"))
+            return codes[:], scales[:]
+
+        for chunk in range(1 + SPLINE_CHUNKS):
+            spline = chunk - 1
+            w_raw = w_raw_pool.tile([P, OUT_TILES, CHUNK_K], BF16)
+            w_dram = fc2_base_w if chunk == 0 else fc2_spline_w[:, spline * CHUNK_K : (spline + 1) * CHUNK_K]
+            nc.sync.dma_start(out=w_raw[:], in_=w_dram.rearrange("(m r) k -> r m k", r=P))
+            for g in range(CHUNK_PASSES):
+                w_codes, w_scales = quantised_weights(w_raw, g)
+                if chunk == 0:
+                    codes, scales = silu_codes[:, g, :], silu_scales[:, g, :]
+                else:
+                    codes, scales = quantised_basis(h_reps[spline], g)
+                for m in range(OUT_TILES):
+                    nc.tensor.matmul_mx(
+                        out=y_ps[m][:],
+                        lhsT=w_codes[:, m * P : (m + 1) * P].bitcast(FP8X4),
+                        lhsT_scale=w_scales[:, m * P : (m + 1) * P],
+                        rhs=codes.bitcast(FP8X4),
+                        rhs_scale=scales,
+                        start=(chunk == 0 and g == 0),
+                        stop=(chunk == SPLINE_CHUNKS and g == CHUNK_PASSES - 1),
+                    )
+            if 1 <= chunk <= SPLINE_CHUNKS - PARKED_CHUNKS:
+                h_reps.append(replicate_hidden(spline + PARKED_CHUNKS))
+
+        for m in range(OUT_TILES):
+            res = res_pool.tile([P, 2, CHANNELS], F32)
+            nc.vector.scalar_tensor_tensor(
+                out=res[:],
+                in0=y_ps[m][:].rearrange("r (b c) -> r b c", b=2),
+                scalar=bias_col[:, m : m + 1],
+                in1=x_sb[:, m : 2 * OUT_TILES : OUT_TILES, :],
+                op0=ALU.add,
+                op1=ALU.add,
+            )
+            nc.sync.dma_start(out=out_tiles[:, m : 2 * OUT_TILES : OUT_TILES, :], in_=res[:])

@@ -24,14 +24,19 @@ CENTRES = 8
 OUT_TILES = 4
 CHANNELS = 256
 
-CHUNK_PASSES = 4
-CHUNK_K = CHUNK_PASSES * K_PASS
-SPLINE_CHUNKS = HIDDEN * CENTRES // CHUNK_K
-CHUNK_HIDDEN = CHUNK_K // CENTRES
+BASE_PASSES = HIDDEN // K_PASS
+SPLINE_PASSES = HIDDEN * CENTRES // K_PASS
+
 COPIES = 4
 GROUP_HIDDEN = P // COPIES
+CHUNK_HIDDEN = 2 * P
 CHUNK_GROUPS = CHUNK_HIDDEN // GROUP_HIDDEN
+CHUNK_PASSES = CHUNK_GROUPS // 2
+CHUNKS = HIDDEN // CHUNK_HIDDEN
 PARKED_CHUNKS = 4
+WEIGHTS_AHEAD = 8
+WEIGHTS_LEAD = 1
+VECTOR_TOKENS = 320
 
 INV_D = 3.5
 
@@ -49,23 +54,32 @@ def tile_kan1_pb_k_kernel(tc, h_mix, x, fc2_spline_w, fc2_base_w, fc2_base_b, ou
     out_rows = out.flatten_outer_dims()
     out_tiles = out_rows.rearrange("(g r) c -> r g c", r=P)
 
+    order = []
+    for g in range(SPLINE_PASSES):
+        order.append(("spline", g))
+        if g % 8 == 3:
+            order.append(("base", g // 8))
+    n_passes = len(order)
+
+    def is_pass(s):
+        return 0 <= s < n_passes
+
+    def is_spline(s):
+        return is_pass(s) and order[s][0] == "spline"
+
     with ExitStack() as stack:
         keep = stack.enter_context(tc.tile_pool(name="keep", bufs=1))
-        w_raw_pool = stack.enter_context(tc.tile_pool(name="w_raw", bufs=3))
+        w_raw_pool = stack.enter_context(tc.tile_pool(name="w_raw", bufs=WEIGHTS_AHEAD))
         w_pool = stack.enter_context(tc.tile_pool(name="w", bufs=2))
-        w_mx_pool = stack.enter_context(tc.tile_pool(name="w_mx", bufs=6))
-        h_t_pool = stack.enter_context(tc.tile_pool(name="h_t", bufs=PARKED_CHUNKS))
+        w_mx_pool = stack.enter_context(tc.tile_pool(name="w_mx", bufs=4 + WEIGHTS_LEAD))
+        h_t_pool = stack.enter_context(tc.tile_pool(name="h_t", bufs=CHUNKS))
         h_rep_pool = stack.enter_context(tc.tile_pool(name="h_rep", bufs=PARKED_CHUNKS))
         act_pool = stack.enter_context(tc.tile_pool(name="act", bufs=2))
         act_mx_pool = stack.enter_context(tc.tile_pool(name="act_mx", bufs=3))
         res_pool = stack.enter_context(tc.tile_pool(name="res", bufs=OUT_TILES))
         y_pool = stack.enter_context(tc.psum_pool(name="y", bufs=1))
         turn_pool = stack.enter_context(tc.psum_pool(name="turn", bufs=4))
-
-        ident_bf = keep.tile([P, P], BF16)
-        make_identity(nc, ident_bf[:])
-        ident_f32 = keep.tile([P, P], F32)
-        make_identity(nc, ident_f32[:])
+        stack.enter_context(tc.manual_schedule())
 
         part_idx = keep.tile([P, 1], I32)
         nc.gpsimd.iota(part_idx[:], pattern=[[0, 1]], base=0, channel_multiplier=1)
@@ -79,9 +93,11 @@ def tile_kan1_pb_k_kernel(tc, h_mix, x, fc2_spline_w, fc2_base_w, fc2_base_b, ou
             nc.vector.tensor_scalar(
                 out=centre[:, e : e + 1], in0=part_mod_f[:], scalar1=2.0, scalar2=e - 3.5, op0=ALU.mult, op1=ALU.add
             )
-            nc.vector.tensor_scalar(
-                out=minus_centre[:, e : e + 1], in0=part_mod_f[:], scalar1=-2.0, scalar2=3.5 - e, op0=ALU.mult, op1=ALU.add
-            )
+        nc.vector.tensor_scalar_mul(out=minus_centre[:], in0=centre[:], scalar1=-1.0)
+        ident_bf = keep.tile([P, P], BF16)
+        make_identity(nc, ident_bf[:])
+        ident_f32 = keep.tile([P, P], F32)
+        make_identity(nc, ident_f32[:])
 
         h_sb = keep.tile([P, TOKEN_TILES, HIDDEN], BF16)
         for quarter in range(4):
@@ -93,7 +109,10 @@ def tile_kan1_pb_k_kernel(tc, h_mix, x, fc2_spline_w, fc2_base_w, fc2_base_b, ou
         nc.vector.memset(bias_rows[:], 0.0)
         nc.gpsimd.dma_start(out=bias_rows[0:OUT_TILES, :], in_=fc2_base_b.rearrange("(m r) -> m r", r=P))
 
-        def replicate_hidden(chunk):
+        h_t = {}
+        h_rep = {}
+
+        def turn_hidden(chunk):
             h_t_ps = turn_pool.tile([P, 2, TOKENS], BF16, tag="turn")
             for half in range(2):
                 first = chunk * CHUNK_HIDDEN + half * P
@@ -101,24 +120,127 @@ def tile_kan1_pb_k_kernel(tc, h_mix, x, fc2_spline_w, fc2_base_w, fc2_base_b, ou
                     nc.tensor.transpose(
                         h_t_ps[:, half, t * P : (t + 1) * P], h_sb[:, t, first : first + P], ident_bf[:]
                     )
-            h_t = h_t_pool.tile([P, 2, TOKENS], BF16)
-            nc.vector.tensor_copy(out=h_t[:], in_=h_t_ps[:])
+            turned = h_t_pool.tile([P, 2, TOKENS], BF16)
+            nc.vector.tensor_copy(out=turned[:], in_=h_t_ps[:])
+            h_t[chunk] = turned
+
+        def parked_rows(chunk):
             first_row = (chunk % PARKED_CHUNKS) * CHUNK_HIDDEN
-            parked = out_rows[first_row : first_row + CHUNK_HIDDEN, :]
-            nc.sync.dma_start(out=parked.rearrange("(a r) w -> r a w", r=P), in_=h_t[:].bitcast(F32))
-            h_rep = h_rep_pool.tile([P, CHUNK_GROUPS, TOKENS], BF16)
+            return out_rows[first_row : first_row + CHUNK_HIDDEN, :]
+
+        def park_hidden(chunk):
+            nc.sync.dma_start(
+                out=parked_rows(chunk).rearrange("(a r) w -> r a w", r=P), in_=h_t[chunk][:].bitcast(F32)
+            )
+
+        def replicate_hidden(chunk):
+            replicated = h_rep_pool.tile([P, CHUNK_GROUPS, TOKENS], BF16)
             for copy in range(COPIES):
                 nc.sync.dma_start(
-                    out=h_rep[copy:P:COPIES, :, :].bitcast(F32),
-                    in_=parked.rearrange("(a r) w -> r a w", r=GROUP_HIDDEN),
+                    out=replicated[copy:P:COPIES, :, :].bitcast(F32),
+                    in_=parked_rows(chunk).rearrange("(a r) w -> r a w", r=GROUP_HIDDEN),
                 )
-            return h_rep
+            h_rep[chunk] = replicated
 
-        h_reps = [replicate_hidden(chunk) for chunk in range(PARKED_CHUNKS)]
+        w_raw = {}
+        w_turned = {}
+        w_grouped = {}
+        w_mx = {}
+        squares = {}
+        basis = {}
+        moving = {}
 
-        silu_codes = keep.tile([P, CHUNK_PASSES, TOKENS], U32, align_bytes=64)
-        silu_scales = keep.tile([P, CHUNK_PASSES, TOKENS], U8, align_bytes=64)
-        for g in range(CHUNK_PASSES):
+        def load_weights(s):
+            kind, g = order[s]
+            w_dram = fc2_base_w if kind == "base" else fc2_spline_w
+            raw = w_raw_pool.tile([P, OUT_TILES, K_PASS], BF16)
+            nc.sync.dma_start(
+                out=raw[:], in_=w_dram[:, g * K_PASS : (g + 1) * K_PASS].rearrange("(m r) k -> r m k", r=P)
+            )
+            w_raw[s] = raw
+
+        def turn_weights(s):
+            banks = []
+            for bank in range(2):
+                w_t_ps = turn_pool.tile([P, 2, 2, P], F32, tag="turn")
+                for m in range(2):
+                    for u in range(2):
+                        nc.tensor.transpose(
+                            w_t_ps[:, m, u, :],
+                            w_raw[s][:, 2 * bank + m, :].bitcast(F32)[:, u * P : (u + 1) * P],
+                            ident_f32[:],
+                        )
+                banks.append(w_t_ps)
+            w_turned[s] = banks
+
+        def group_weights(s):
+            w_bf = w_pool.tile([P, OUT_TILES * P * PACK], BF16, align_bytes=64)
+            w_words = w_bf[:].bitcast(F32).rearrange("q (b m r u) -> q b m r u", b=2, m=2, u=2)
+            for bank in range(2):
+                nc.vector.tensor_copy(out=w_words[:, bank], in_=w_turned[s][bank][:].rearrange("q m u r -> q m r u"))
+            w_grouped[s] = w_bf
+
+        def quantise_weights(s):
+            w_codes = w_mx_pool.tile([P, OUT_TILES * P], U32, align_bytes=64)
+            w_scales = w_mx_pool.tile([P, OUT_TILES * P], U8, align_bytes=64)
+            quantise(nc, w_codes[:], w_scales[:], w_grouped[s][:])
+            w_mx[s] = (w_codes, w_scales)
+
+        def square_offsets(s):
+            g = order[s][1]
+            first = 2 * (g % CHUNK_PASSES)
+            h_pair = h_rep[g // CHUNK_PASSES][:, first : first + 2, :].rearrange("q u n -> q n u")
+            square = act_pool.tile([P, 2, TOKENS, 2], F32)
+            offset = act_pool.tile([P, VECTOR_TOKENS, 2], F32)
+            nc.vector.tensor_scalar(
+                out=offset[:],
+                in0=h_pair[:, 0:VECTOR_TOKENS, :],
+                scalar1=INV_D,
+                scalar2=centre[:, 0:1],
+                op0=ALU.mult,
+                op1=ALU.subtract,
+            )
+            nc.vector.tensor_tensor(out=square[:, 0, 0:VECTOR_TOKENS, :], in0=offset[:], in1=offset[:], op=ALU.mult)
+            for e, first_token in ((1, 0), (0, VECTOR_TOKENS)):
+                nc.scalar.activation(
+                    out=square[:, e, first_token:TOKENS, :],
+                    in_=h_pair[:, first_token:TOKENS, :],
+                    func=ACT.Square,
+                    scale=INV_D,
+                    bias=minus_centre[:, e : e + 1],
+                )
+            squares[s] = square
+
+        def exponentials(s):
+            basis_bf = act_pool.tile([P, TOKENS * 2, 2], BF16, align_bytes=64)
+            nc.scalar.activation(
+                out=basis_bf[:], in_=squares[s][:].rearrange("q e n u -> q (n u) e"), func=ACT.Exp, scale=-1.0
+            )
+            basis[s] = basis_bf
+
+        def quantise_basis(s):
+            codes = act_mx_pool.tile([P, TOKENS], U32, align_bytes=64)
+            scales = act_mx_pool.tile([P, TOKENS], U8, align_bytes=64)
+            quantise(nc, codes[:], scales[:], basis[s][:].rearrange("q n e -> q (n e)"))
+            moving[s] = (codes[:], scales[:])
+
+        def multiply(s):
+            w_codes, w_scales = w_mx[s]
+            codes, scales = moving[s]
+            for m in range(OUT_TILES):
+                nc.tensor.matmul_mx(
+                    out=y_ps[m][:],
+                    lhsT=w_codes[:, m * P : (m + 1) * P].bitcast(FP8X4),
+                    lhsT_scale=w_scales[:, m * P : (m + 1) * P],
+                    rhs=codes.bitcast(FP8X4),
+                    rhs_scale=scales,
+                    start=(s == 0),
+                    stop=(s == n_passes - 1),
+                )
+
+        silu_codes = keep.tile([P, BASE_PASSES, TOKENS], U32, align_bytes=64)
+        silu_scales = keep.tile([P, BASE_PASSES, TOKENS], U8, align_bytes=64)
+        for g in range(BASE_PASSES):
             silu_bf = act_pool.tile([P, TOKENS, PACK], BF16, align_bytes=64)
             for half in range(2):
                 h_w_ps = turn_pool.tile([P, 2, 2 * P], F32, tag="turn")
@@ -135,7 +257,16 @@ def tile_kan1_pb_k_kernel(tc, h_mix, x, fc2_spline_w, fc2_base_w, fc2_base_b, ou
                     in_=h_w_ps[:].bitcast(BF16).rearrange("q u (n e) -> q n u e", e=2),
                     func=ACT.Silu,
                 )
+            turn_hidden(2 * g)
+            turn_hidden(2 * g + 1)
             quantise(nc, silu_codes[:, g, :], silu_scales[:, g, :], silu_bf[:].rearrange("q n t -> q (n t)"))
+            moving[order.index(("base", g))] = (silu_codes[:, g, :], silu_scales[:, g, :])
+
+        for chunk in range(PARKED_CHUNKS):
+            park_hidden(chunk)
+            load_weights(2 * chunk)
+            load_weights(2 * chunk + 1)
+            replicate_hidden(chunk)
 
         bias_ps = turn_pool.tile([P, P], BF16, tag="turn")
         nc.tensor.transpose(bias_ps[:], bias_rows[:], ident_bf[:])
@@ -144,77 +275,29 @@ def tile_kan1_pb_k_kernel(tc, h_mix, x, fc2_spline_w, fc2_base_w, fc2_base_b, ou
 
         y_ps = [y_pool.tile([P, TOKENS], F32, name="y_ps%d" % m) for m in range(OUT_TILES)]
 
-        def quantised_weights(w_raw, g):
-            w_bf = w_pool.tile([P, OUT_TILES * P * PACK], BF16, align_bytes=64)
-            w_words = w_bf[:].bitcast(F32).rearrange("q (b m n u) -> q b m n u", b=2, m=2, u=2)
-            for bank in range(2):
-                w_t_ps = turn_pool.tile([P, 2, 2, P], F32, tag="turn")
-                for m in range(2):
-                    for u in range(2):
-                        first = g * WORDS + u * P
-                        nc.tensor.transpose(
-                            w_t_ps[:, m, u, :],
-                            w_raw[:, 2 * bank + m, :].bitcast(F32)[:, first : first + P],
-                            ident_f32[:],
-                        )
-                source = w_t_ps[:].rearrange("q m u n -> q m n u")
-                if bank == 0:
-                    nc.scalar.copy(out=w_words[:, bank], in_=source)
-                else:
-                    nc.vector.tensor_copy(out=w_words[:, bank], in_=source)
-            w_codes = w_mx_pool.tile([P, OUT_TILES * P], U32, align_bytes=64)
-            w_scales = w_mx_pool.tile([P, OUT_TILES * P], U8, align_bytes=64)
-            quantise(nc, w_codes[:], w_scales[:], w_bf[:])
-            return w_codes, w_scales
-
-        def quantised_basis(h_rep, g):
-            h_pair = h_rep[:, 2 * g : 2 * g + 2, :].rearrange("q u n -> q n u")
-            square = act_pool.tile([P, 2, TOKENS * 2], F32)
-            offset = act_pool.tile([P, TOKENS, 2], F32)
-            nc.vector.tensor_scalar(
-                out=offset[:], in0=h_pair, scalar1=INV_D, scalar2=centre[:, 0:1], op0=ALU.mult, op1=ALU.subtract
-            )
-            offset_flat = offset[:].rearrange("q n u -> q (n u)")
-            nc.vector.tensor_tensor(out=square[:, 0, :], in0=offset_flat, in1=offset_flat, op=ALU.mult)
-            nc.scalar.activation(
-                out=square[:, 1, :].rearrange("q (n u) -> q n u", u=2),
-                in_=h_pair,
-                func=ACT.Square,
-                scale=INV_D,
-                bias=minus_centre[:, 1:2],
-            )
-            basis_bf = act_pool.tile([P, TOKENS * 2, 2], BF16, align_bytes=64)
-            nc.scalar.activation(
-                out=basis_bf[:], in_=square[:].rearrange("q e n -> q n e"), func=ACT.Exp, scale=-1.0
-            )
-            codes = act_mx_pool.tile([P, TOKENS], U32, align_bytes=64)
-            scales = act_mx_pool.tile([P, TOKENS], U8, align_bytes=64)
-            quantise(nc, codes[:], scales[:], basis_bf[:].rearrange("q n e -> q (n e)"))
-            return codes[:], scales[:]
-
-        for chunk in range(1 + SPLINE_CHUNKS):
-            spline = chunk - 1
-            w_raw = w_raw_pool.tile([P, OUT_TILES, CHUNK_K], BF16)
-            w_dram = fc2_base_w if chunk == 0 else fc2_spline_w[:, spline * CHUNK_K : (spline + 1) * CHUNK_K]
-            nc.sync.dma_start(out=w_raw[:], in_=w_dram.rearrange("(m r) k -> r m k", r=P))
-            for g in range(CHUNK_PASSES):
-                w_codes, w_scales = quantised_weights(w_raw, g)
-                if chunk == 0:
-                    codes, scales = silu_codes[:, g, :], silu_scales[:, g, :]
-                else:
-                    codes, scales = quantised_basis(h_reps[spline], g)
-                for m in range(OUT_TILES):
-                    nc.tensor.matmul_mx(
-                        out=y_ps[m][:],
-                        lhsT=w_codes[:, m * P : (m + 1) * P].bitcast(FP8X4),
-                        lhsT_scale=w_scales[:, m * P : (m + 1) * P],
-                        rhs=codes.bitcast(FP8X4),
-                        rhs_scale=scales,
-                        start=(chunk == 0 and g == 0),
-                        stop=(chunk == SPLINE_CHUNKS and g == CHUNK_PASSES - 1),
-                    )
-            if 1 <= chunk <= SPLINE_CHUNKS - PARKED_CHUNKS:
-                h_reps.append(replicate_hidden(spline + PARKED_CHUNKS))
+        for step in range(-3 - WEIGHTS_LEAD, n_passes + 2):
+            ahead = step + WEIGHTS_LEAD
+            if is_spline(step - 1):
+                quantise_basis(step - 1)
+            if is_pass(step - 1):
+                multiply(step - 1)
+            if is_spline(step + 1):
+                square_offsets(step + 1)
+                g = order[step + 1][1]
+                refill = g // CHUNK_PASSES + PARKED_CHUNKS
+                if g % CHUNK_PASSES == CHUNK_PASSES - 1 and refill < CHUNKS:
+                    park_hidden(refill)
+                    replicate_hidden(refill)
+            if is_spline(step):
+                exponentials(step)
+            if is_pass(ahead + 3):
+                turn_weights(ahead + 3)
+                if is_pass(ahead + 3 + WEIGHTS_AHEAD):
+                    load_weights(ahead + 3 + WEIGHTS_AHEAD)
+            if is_pass(ahead + 2):
+                group_weights(ahead + 2)
+            if is_pass(ahead + 1):
+                quantise_weights(ahead + 1)
 
         for m in range(OUT_TILES):
             res = res_pool.tile([P, 2, CHANNELS], F32)

@@ -146,6 +146,7 @@ def tile_kan1_pb_k_kernel(tc, h_mix, x, fc2_spline_w, fc2_base_w, fc2_base_b, ou
         w_turned = {}
         w_grouped = {}
         w_mx = {}
+        offsets = {}
         squares = {}
         basis = {}
         moving = {}
@@ -186,21 +187,31 @@ def tile_kan1_pb_k_kernel(tc, h_mix, x, fc2_spline_w, fc2_base_w, fc2_base_b, ou
             quantise(nc, w_codes[:], w_scales[:], w_grouped[s][:])
             w_mx[s] = (w_codes, w_scales)
 
-        def square_offsets(s):
+        def hidden_pair(s):
             g = order[s][1]
             first = 2 * (g % CHUNK_PASSES)
-            h_pair = h_rep[g // CHUNK_PASSES][:, first : first + 2, :].rearrange("q u n -> q n u")
-            square = act_pool.tile([P, 2, TOKENS, 2], F32)
+            return h_rep[g // CHUNK_PASSES][:, first : first + 2, :].rearrange("q u n -> q n u")
+
+        def vector_offsets(s):
             offset = act_pool.tile([P, VECTOR_TOKENS, 2], F32)
             nc.vector.tensor_scalar(
                 out=offset[:],
-                in0=h_pair[:, 0:VECTOR_TOKENS, :],
+                in0=hidden_pair(s)[:, 0:VECTOR_TOKENS, :],
                 scalar1=INV_D,
                 scalar2=centre[:, 0:1],
                 op0=ALU.mult,
                 op1=ALU.subtract,
             )
-            nc.vector.tensor_tensor(out=square[:, 0, 0:VECTOR_TOKENS, :], in0=offset[:], in1=offset[:], op=ALU.mult)
+            offsets[s] = offset
+
+        def vector_squares(s):
+            nc.vector.tensor_tensor(
+                out=squares[s][:, 0, 0:VECTOR_TOKENS, :], in0=offsets[s][:], in1=offsets[s][:], op=ALU.mult
+            )
+
+        def scalar_squares(s):
+            h_pair = hidden_pair(s)
+            square = act_pool.tile([P, 2, TOKENS, 2], F32)
             for e, first_token in ((1, 0), (0, VECTOR_TOKENS)):
                 nc.scalar.activation(
                     out=square[:, e, first_token:TOKENS, :],
@@ -282,7 +293,8 @@ def tile_kan1_pb_k_kernel(tc, h_mix, x, fc2_spline_w, fc2_base_w, fc2_base_b, ou
             if is_pass(step - 1):
                 multiply(step - 1)
             if is_spline(step + 1):
-                square_offsets(step + 1)
+                vector_offsets(step + 1)
+                scalar_squares(step + 1)
                 g = order[step + 1][1]
                 refill = g // CHUNK_PASSES + PARKED_CHUNKS
                 if g % CHUNK_PASSES == CHUNK_PASSES - 1 and refill < CHUNKS:
@@ -296,6 +308,8 @@ def tile_kan1_pb_k_kernel(tc, h_mix, x, fc2_spline_w, fc2_base_w, fc2_base_b, ou
                     load_weights(ahead + 3 + WEIGHTS_AHEAD)
             if is_pass(ahead + 2):
                 group_weights(ahead + 2)
+            if is_spline(step + 1):
+                vector_squares(step + 1)
             if is_pass(ahead + 1):
                 quantise_weights(ahead + 1)
 

@@ -24,18 +24,21 @@ CENTRES = 8
 OUT_TILES = 4
 CHANNELS = 256
 
+ROUND_PASSES = 2
+ROUND_K = ROUND_PASSES * K_PASS
 BASE_PASSES = HIDDEN // K_PASS
-SPLINE_PASSES = HIDDEN * CENTRES // K_PASS
+BASE_ROUNDS = BASE_PASSES // ROUND_PASSES
+SPLINE_ROUNDS = HIDDEN * CENTRES // ROUND_K
 
 COPIES = 4
 GROUP_HIDDEN = P // COPIES
 CHUNK_HIDDEN = 2 * P
 CHUNK_GROUPS = CHUNK_HIDDEN // GROUP_HIDDEN
-CHUNK_PASSES = CHUNK_GROUPS // 2
+ROUND_GROUPS = 2 * ROUND_PASSES
+CHUNK_ROUNDS = CHUNK_GROUPS // ROUND_GROUPS
 CHUNKS = HIDDEN // CHUNK_HIDDEN
-PARKED_CHUNKS = 4
-WEIGHTS_AHEAD = 8
-WEIGHTS_LEAD = 1
+PARKED_CHUNKS = 3
+WEIGHTS_AHEAD = 4
 VECTOR_TOKENS = 320
 
 INV_D = 3.5
@@ -55,27 +58,27 @@ def tile_kan1_pb_k_kernel(tc, h_mix, x, fc2_spline_w, fc2_base_w, fc2_base_b, ou
     out_tiles = out_rows.rearrange("(g r) c -> r g c", r=P)
 
     order = []
-    for g in range(SPLINE_PASSES):
-        order.append(("spline", g))
-        if g % 8 == 3:
-            order.append(("base", g // 8))
-    n_passes = len(order)
+    for r in range(SPLINE_ROUNDS):
+        order.append(("spline", r))
+        if r % 8 == 1:
+            order.append(("base", r // 8))
+    n_rounds = len(order)
 
-    def is_pass(s):
-        return 0 <= s < n_passes
+    def is_round(i):
+        return 0 <= i < n_rounds
 
-    def is_spline(s):
-        return is_pass(s) and order[s][0] == "spline"
+    def is_spline(i):
+        return is_round(i) and order[i][0] == "spline"
 
     with ExitStack() as stack:
         keep = stack.enter_context(tc.tile_pool(name="keep", bufs=1))
         w_raw_pool = stack.enter_context(tc.tile_pool(name="w_raw", bufs=WEIGHTS_AHEAD))
         w_pool = stack.enter_context(tc.tile_pool(name="w", bufs=2))
-        w_mx_pool = stack.enter_context(tc.tile_pool(name="w_mx", bufs=4 + WEIGHTS_LEAD))
+        w_mx_pool = stack.enter_context(tc.tile_pool(name="w_mx", bufs=3))
         h_t_pool = stack.enter_context(tc.tile_pool(name="h_t", bufs=CHUNKS))
         h_rep_pool = stack.enter_context(tc.tile_pool(name="h_rep", bufs=PARKED_CHUNKS))
         act_pool = stack.enter_context(tc.tile_pool(name="act", bufs=2))
-        act_mx_pool = stack.enter_context(tc.tile_pool(name="act_mx", bufs=3))
+        act_mx_pool = stack.enter_context(tc.tile_pool(name="act_mx", bufs=2))
         res_pool = stack.enter_context(tc.tile_pool(name="res", bufs=OUT_TILES))
         y_pool = stack.enter_context(tc.psum_pool(name="y", bufs=1))
         turn_pool = stack.enter_context(tc.psum_pool(name="turn", bufs=4))
@@ -99,10 +102,12 @@ def tile_kan1_pb_k_kernel(tc, h_mix, x, fc2_spline_w, fc2_base_w, fc2_base_b, ou
         ident_f32 = keep.tile([P, P], F32)
         make_identity(nc, ident_f32[:])
 
-        h_sb = keep.tile([P, TOKEN_TILES, HIDDEN], BF16)
-        for quarter in range(4):
+        h_sb = []
+        for quarter in range(BASE_PASSES):
+            h_quarter = keep.tile([P, TOKEN_TILES, K_PASS], BF16, name="h_quarter%d" % quarter)
             cols = slice(quarter * K_PASS, (quarter + 1) * K_PASS)
-            nc.sync.dma_start(out=h_sb[:, :, cols], in_=h_rows[:, cols].rearrange("(t r) j -> r t j", r=P))
+            nc.sync.dma_start(out=h_quarter[:], in_=h_rows[:, cols].rearrange("(t r) j -> r t j", r=P))
+            h_sb.append(h_quarter)
         x_sb = keep.tile([P, 2 * OUT_TILES, CHANNELS], BF16)
         nc.gpsimd.dma_start(out=x_sb[:], in_=x_rows)
         bias_rows = keep.tile([P, P], BF16)
@@ -114,11 +119,12 @@ def tile_kan1_pb_k_kernel(tc, h_mix, x, fc2_spline_w, fc2_base_w, fc2_base_b, ou
 
         def turn_hidden(chunk):
             h_t_ps = turn_pool.tile([P, 2, TOKENS], BF16, tag="turn")
+            quarter, first_hidden = divmod(chunk * CHUNK_HIDDEN, K_PASS)
             for half in range(2):
-                first = chunk * CHUNK_HIDDEN + half * P
+                first = first_hidden + half * P
                 for t in range(TOKEN_TILES):
                     nc.tensor.transpose(
-                        h_t_ps[:, half, t * P : (t + 1) * P], h_sb[:, t, first : first + P], ident_bf[:]
+                        h_t_ps[:, half, t * P : (t + 1) * P], h_sb[quarter][:, t, first : first + P], ident_bf[:]
                     )
             turned = h_t_pool.tile([P, 2, TOKENS], BF16)
             nc.vector.tensor_copy(out=turned[:], in_=h_t_ps[:])
@@ -146,108 +152,106 @@ def tile_kan1_pb_k_kernel(tc, h_mix, x, fc2_spline_w, fc2_base_w, fc2_base_b, ou
         w_turned = {}
         w_grouped = {}
         w_mx = {}
-        offsets = {}
         squares = {}
         basis = {}
         moving = {}
 
-        def load_weights(s):
-            kind, g = order[s]
+        def load_weights(i):
+            kind, r = order[i]
             w_dram = fc2_base_w if kind == "base" else fc2_spline_w
-            raw = w_raw_pool.tile([P, OUT_TILES, K_PASS], BF16)
+            raw = w_raw_pool.tile([P, OUT_TILES, ROUND_K], BF16)
             nc.sync.dma_start(
-                out=raw[:], in_=w_dram[:, g * K_PASS : (g + 1) * K_PASS].rearrange("(m r) k -> r m k", r=P)
+                out=raw[:], in_=w_dram[:, r * ROUND_K : (r + 1) * ROUND_K].rearrange("(m r) k -> r m k", r=P)
             )
-            w_raw[s] = raw
+            w_raw[i] = raw
 
-        def turn_weights(s):
+        def turn_weights(i):
             banks = []
-            for bank in range(2):
-                w_t_ps = turn_pool.tile([P, 2, 2, P], F32, tag="turn")
-                for m in range(2):
-                    for u in range(2):
-                        nc.tensor.transpose(
-                            w_t_ps[:, m, u, :],
-                            w_raw[s][:, 2 * bank + m, :].bitcast(F32)[:, u * P : (u + 1) * P],
-                            ident_f32[:],
-                        )
-                banks.append(w_t_ps)
-            w_turned[s] = banks
+            for a in range(ROUND_PASSES):
+                for half in range(2):
+                    w_t_ps = turn_pool.tile([P, 2, 2, P], F32, tag="turn")
+                    for m in range(2):
+                        for u in range(2):
+                            first = a * WORDS + u * P
+                            nc.tensor.transpose(
+                                w_t_ps[:, m, u, :],
+                                w_raw[i][:, 2 * half + m, :].bitcast(F32)[:, first : first + P],
+                                ident_f32[:],
+                            )
+                    banks.append(w_t_ps)
+            w_turned[i] = banks
 
-        def group_weights(s):
-            w_bf = w_pool.tile([P, OUT_TILES * P * PACK], BF16, align_bytes=64)
-            w_words = w_bf[:].bitcast(F32).rearrange("q (b m r u) -> q b m r u", b=2, m=2, u=2)
-            for bank in range(2):
-                nc.vector.tensor_copy(out=w_words[:, bank], in_=w_turned[s][bank][:].rearrange("q m u r -> q m r u"))
-            w_grouped[s] = w_bf
+        def group_weights(i):
+            w_bf = w_pool.tile([P, ROUND_PASSES * OUT_TILES * P * PACK], BF16, align_bytes=64)
+            w_words = w_bf[:].bitcast(F32).rearrange("q (b m r u) -> q b m r u", m=2, r=P, u=2)
+            for bank in range(2 * ROUND_PASSES):
+                nc.vector.tensor_copy(out=w_words[:, bank], in_=w_turned[i][bank][:].rearrange("q m u r -> q m r u"))
+            w_grouped[i] = w_bf
 
-        def quantise_weights(s):
-            w_codes = w_mx_pool.tile([P, OUT_TILES * P], U32, align_bytes=64)
-            w_scales = w_mx_pool.tile([P, OUT_TILES * P], U8, align_bytes=64)
-            quantise(nc, w_codes[:], w_scales[:], w_grouped[s][:])
-            w_mx[s] = (w_codes, w_scales)
+        def quantise_weights(i):
+            w_codes = w_mx_pool.tile([P, ROUND_PASSES * OUT_TILES * P], U32, align_bytes=64)
+            w_scales = w_mx_pool.tile([P, ROUND_PASSES * OUT_TILES * P], U8, align_bytes=64)
+            quantise(nc, w_codes[:], w_scales[:], w_grouped[i][:])
+            w_mx[i] = (w_codes, w_scales)
 
-        def hidden_pair(s):
-            g = order[s][1]
-            first = 2 * (g % CHUNK_PASSES)
-            return h_rep[g // CHUNK_PASSES][:, first : first + 2, :].rearrange("q u n -> q n u")
-
-        def vector_offsets(s):
-            offset = act_pool.tile([P, VECTOR_TOKENS, 2], F32)
+        def square_offsets(i):
+            r = order[i][1]
+            first = ROUND_GROUPS * (r % CHUNK_ROUNDS)
+            h_round = h_rep[r // CHUNK_ROUNDS][:, first : first + ROUND_GROUPS, :].rearrange("q (a u) n -> q a n u", u=2)
+            square = act_pool.tile([P, 2, ROUND_PASSES, TOKENS, 2], F32)
+            offset = act_pool.tile([P, ROUND_PASSES, VECTOR_TOKENS, 2], F32)
             nc.vector.tensor_scalar(
                 out=offset[:],
-                in0=hidden_pair(s)[:, 0:VECTOR_TOKENS, :],
+                in0=h_round[:, :, 0:VECTOR_TOKENS, :],
                 scalar1=INV_D,
                 scalar2=centre[:, 0:1],
                 op0=ALU.mult,
                 op1=ALU.subtract,
             )
-            offsets[s] = offset
-
-        def vector_squares(s):
-            nc.vector.tensor_tensor(
-                out=squares[s][:, 0, 0:VECTOR_TOKENS, :], in0=offsets[s][:], in1=offsets[s][:], op=ALU.mult
-            )
-
-        def scalar_squares(s):
-            h_pair = hidden_pair(s)
-            square = act_pool.tile([P, 2, TOKENS, 2], F32)
+            nc.vector.tensor_tensor(out=square[:, 0, :, 0:VECTOR_TOKENS, :], in0=offset[:], in1=offset[:], op=ALU.mult)
             for e, first_token in ((1, 0), (0, VECTOR_TOKENS)):
                 nc.scalar.activation(
-                    out=square[:, e, first_token:TOKENS, :],
-                    in_=h_pair[:, first_token:TOKENS, :],
+                    out=square[:, e, :, first_token:TOKENS, :],
+                    in_=h_round[:, :, first_token:TOKENS, :],
                     func=ACT.Square,
                     scale=INV_D,
                     bias=minus_centre[:, e : e + 1],
                 )
-            squares[s] = square
+            squares[i] = square
 
-        def exponentials(s):
-            basis_bf = act_pool.tile([P, TOKENS * 2, 2], BF16, align_bytes=64)
+        def exponentials(i):
+            basis_bf = act_pool.tile([P, ROUND_PASSES * TOKENS * 2, 2], BF16, align_bytes=64)
             nc.scalar.activation(
-                out=basis_bf[:], in_=squares[s][:].rearrange("q e n u -> q (n u) e"), func=ACT.Exp, scale=-1.0
+                out=basis_bf[:], in_=squares[i][:].rearrange("q e a n u -> q (a n u) e"), func=ACT.Exp, scale=-1.0
             )
-            basis[s] = basis_bf
+            basis[i] = basis_bf
 
-        def quantise_basis(s):
-            codes = act_mx_pool.tile([P, TOKENS], U32, align_bytes=64)
-            scales = act_mx_pool.tile([P, TOKENS], U8, align_bytes=64)
-            quantise(nc, codes[:], scales[:], basis[s][:].rearrange("q n e -> q (n e)"))
-            moving[s] = (codes[:], scales[:])
+        def quantise_basis(i):
+            codes = act_mx_pool.tile([P, ROUND_PASSES, TOKENS], U32, align_bytes=64)
+            scales = act_mx_pool.tile([P, ROUND_PASSES, TOKENS], U8, align_bytes=64)
+            quantise(
+                nc,
+                codes[:].rearrange("q a n -> q (a n)"),
+                scales[:].rearrange("q a n -> q (a n)"),
+                basis[i][:].rearrange("q n e -> q (n e)"),
+            )
+            moving[i] = (codes[:], scales[:])
 
-        def multiply(s):
-            w_codes, w_scales = w_mx[s]
-            codes, scales = moving[s]
+        def multiply(i):
+            w_codes, w_scales = w_mx[i]
+            codes, scales = moving[i]
             for m in range(OUT_TILES):
-                nc.tensor.matmul_mx(
-                    out=y_ps[m][:],
-                    lhsT=w_codes[:, m * P : (m + 1) * P].bitcast(FP8X4),
-                    lhsT_scale=w_scales[:, m * P : (m + 1) * P],
-                    rhs=codes.bitcast(FP8X4),
-                    rhs_scale=scales,
-                    start=(s == 0),
-                    stop=(s == n_passes - 1),
-                )
+                for a in range(ROUND_PASSES):
+                    cols = slice((a * OUT_TILES + m) * P, (a * OUT_TILES + m + 1) * P)
+                    nc.tensor.matmul_mx(
+                        out=y_ps[m][:],
+                        lhsT=w_codes[:, cols].bitcast(FP8X4),
+                        lhsT_scale=w_scales[:, cols],
+                        rhs=codes[:, a, :].bitcast(FP8X4),
+                        rhs_scale=scales[:, a, :],
+                        start=(i == 0 and a == 0),
+                        stop=(i == n_rounds - 1 and a == ROUND_PASSES - 1),
+                    )
 
         silu_codes = keep.tile([P, BASE_PASSES, TOKENS], U32, align_bytes=64)
         silu_scales = keep.tile([P, BASE_PASSES, TOKENS], U8, align_bytes=64)
@@ -256,11 +260,10 @@ def tile_kan1_pb_k_kernel(tc, h_mix, x, fc2_spline_w, fc2_base_w, fc2_base_b, ou
             for half in range(2):
                 h_w_ps = turn_pool.tile([P, 2, 2 * P], F32, tag="turn")
                 for u in range(2):
-                    first = g * WORDS + u * P
                     for t in range(2):
                         nc.tensor.transpose(
                             h_w_ps[:, u, t * P : (t + 1) * P],
-                            h_sb[:, 2 * half + t, :].bitcast(F32)[:, first : first + P],
+                            h_sb[g][:, 2 * half + t, :].bitcast(F32)[:, u * P : (u + 1) * P],
                             ident_f32[:],
                         )
                 nc.scalar.activation(
@@ -271,13 +274,17 @@ def tile_kan1_pb_k_kernel(tc, h_mix, x, fc2_spline_w, fc2_base_w, fc2_base_b, ou
             turn_hidden(2 * g)
             turn_hidden(2 * g + 1)
             quantise(nc, silu_codes[:, g, :], silu_scales[:, g, :], silu_bf[:].rearrange("q n t -> q (n t)"))
-            moving[order.index(("base", g))] = (silu_codes[:, g, :], silu_scales[:, g, :])
+
+        for b in range(BASE_ROUNDS):
+            passes = slice(b * ROUND_PASSES, (b + 1) * ROUND_PASSES)
+            moving[order.index(("base", b))] = (silu_codes[:, passes, :], silu_scales[:, passes, :])
 
         for chunk in range(PARKED_CHUNKS):
             park_hidden(chunk)
-            load_weights(2 * chunk)
-            load_weights(2 * chunk + 1)
+            load_weights(chunk)
             replicate_hidden(chunk)
+        for i in range(PARKED_CHUNKS, WEIGHTS_AHEAD):
+            load_weights(i)
 
         bias_ps = turn_pool.tile([P, P], BF16, tag="turn")
         nc.tensor.transpose(bias_ps[:], bias_rows[:], ident_bf[:])
@@ -286,32 +293,28 @@ def tile_kan1_pb_k_kernel(tc, h_mix, x, fc2_spline_w, fc2_base_w, fc2_base_b, ou
 
         y_ps = [y_pool.tile([P, TOKENS], F32, name="y_ps%d" % m) for m in range(OUT_TILES)]
 
-        for step in range(-3 - WEIGHTS_LEAD, n_passes + 2):
-            ahead = step + WEIGHTS_LEAD
+        for step in range(-2, n_rounds + 2):
             if is_spline(step - 1):
                 quantise_basis(step - 1)
-            if is_pass(step - 1):
+            if is_round(step - 1):
                 multiply(step - 1)
             if is_spline(step + 1):
-                vector_offsets(step + 1)
-                scalar_squares(step + 1)
-                g = order[step + 1][1]
-                refill = g // CHUNK_PASSES + PARKED_CHUNKS
-                if g % CHUNK_PASSES == CHUNK_PASSES - 1 and refill < CHUNKS:
+                square_offsets(step + 1)
+                r = order[step + 1][1]
+                refill = r // CHUNK_ROUNDS + PARKED_CHUNKS
+                if r % CHUNK_ROUNDS == CHUNK_ROUNDS - 1 and refill < CHUNKS:
                     park_hidden(refill)
                     replicate_hidden(refill)
             if is_spline(step):
                 exponentials(step)
-            if is_pass(ahead + 3):
-                turn_weights(ahead + 3)
-                if is_pass(ahead + 3 + WEIGHTS_AHEAD):
-                    load_weights(ahead + 3 + WEIGHTS_AHEAD)
-            if is_pass(ahead + 2):
-                group_weights(ahead + 2)
-            if is_spline(step + 1):
-                vector_squares(step + 1)
-            if is_pass(ahead + 1):
-                quantise_weights(ahead + 1)
+            if is_round(step + 1):
+                group_weights(step + 1)
+            if is_round(step + 2):
+                turn_weights(step + 2)
+                if is_round(step + 2 + WEIGHTS_AHEAD):
+                    load_weights(step + 2 + WEIGHTS_AHEAD)
+            if is_round(step):
+                quantise_weights(step)
 
         for m in range(OUT_TILES):
             res = res_pool.tile([P, 2, CHANNELS], F32)

@@ -38,8 +38,8 @@ ROUND_GROUPS = 2 * ROUND_PASSES
 CHUNK_ROUNDS = CHUNK_GROUPS // ROUND_GROUPS
 CHUNKS = HIDDEN // CHUNK_HIDDEN
 PARKED_CHUNKS = 3
-WEIGHTS_AHEAD = 4
-VECTOR_TOKENS = 320
+WEIGHTS_AHEAD = 3
+VECTOR_TOKENS = 448
 
 INV_D = 3.5
 
@@ -78,6 +78,7 @@ def tile_kan1_pb_k_kernel(tc, h_mix, x, fc2_spline_w, fc2_base_w, fc2_base_b, ou
         h_t_pool = stack.enter_context(tc.tile_pool(name="h_t", bufs=CHUNKS))
         h_rep_pool = stack.enter_context(tc.tile_pool(name="h_rep", bufs=PARKED_CHUNKS))
         act_pool = stack.enter_context(tc.tile_pool(name="act", bufs=2))
+        offset_pool = stack.enter_context(tc.tile_pool(name="offset", bufs=2))
         act_mx_pool = stack.enter_context(tc.tile_pool(name="act_mx", bufs=2))
         res_pool = stack.enter_context(tc.tile_pool(name="res", bufs=OUT_TILES))
         y_pool = stack.enter_context(tc.psum_pool(name="y", bufs=1))
@@ -90,13 +91,11 @@ def tile_kan1_pb_k_kernel(tc, h_mix, x, fc2_spline_w, fc2_base_w, fc2_base_b, ou
         nc.vector.tensor_single_scalar(out=part_mod[:], in_=part_idx[:], scalar=COPIES - 1, op=ALU.bitwise_and)
         part_mod_f = keep.tile([P, 1], F32)
         nc.vector.tensor_copy(out=part_mod_f[:], in_=part_mod[:])
-        centre = keep.tile([P, 2], F32)
         minus_centre = keep.tile([P, 2], F32)
         for e in range(2):
             nc.vector.tensor_scalar(
-                out=centre[:, e : e + 1], in0=part_mod_f[:], scalar1=2.0, scalar2=e - 3.5, op0=ALU.mult, op1=ALU.add
+                out=minus_centre[:, e : e + 1], in0=part_mod_f[:], scalar1=-2.0, scalar2=3.5 - e, op0=ALU.mult, op1=ALU.add
             )
-        nc.vector.tensor_scalar_mul(out=minus_centre[:], in0=centre[:], scalar1=-1.0)
         ident_bf = keep.tile([P, P], BF16)
         make_identity(nc, ident_bf[:])
         ident_f32 = keep.tile([P, P], F32)
@@ -152,6 +151,7 @@ def tile_kan1_pb_k_kernel(tc, h_mix, x, fc2_spline_w, fc2_base_w, fc2_base_b, ou
         w_turned = {}
         w_grouped = {}
         w_mx = {}
+        offsets = {}
         squares = {}
         basis = {}
         moving = {}
@@ -194,21 +194,29 @@ def tile_kan1_pb_k_kernel(tc, h_mix, x, fc2_spline_w, fc2_base_w, fc2_base_b, ou
             quantise(nc, w_codes[:], w_scales[:], w_grouped[i][:])
             w_mx[i] = (w_codes, w_scales)
 
-        def square_offsets(i):
+        def hidden_of_round(i):
             r = order[i][1]
             first = ROUND_GROUPS * (r % CHUNK_ROUNDS)
-            h_round = h_rep[r // CHUNK_ROUNDS][:, first : first + ROUND_GROUPS, :].rearrange("q (a u) n -> q a n u", u=2)
-            square = act_pool.tile([P, 2, ROUND_PASSES, TOKENS, 2], F32)
-            offset = act_pool.tile([P, ROUND_PASSES, VECTOR_TOKENS, 2], F32)
-            nc.vector.tensor_scalar(
+            return h_rep[r // CHUNK_ROUNDS][:, first : first + ROUND_GROUPS, :].rearrange("q (a u) n -> q a n u", u=2)
+
+        def offsets_from_centre(i):
+            offset = offset_pool.tile([P, ROUND_PASSES, VECTOR_TOKENS, 2], F32)
+            nc.gpsimd.tensor_scalar(
                 out=offset[:],
-                in0=h_round[:, :, 0:VECTOR_TOKENS, :],
+                in0=hidden_of_round(i)[:, :, 0:VECTOR_TOKENS, :],
                 scalar1=INV_D,
-                scalar2=centre[:, 0:1],
+                scalar2=minus_centre[:, 0:1],
                 op0=ALU.mult,
-                op1=ALU.subtract,
+                op1=ALU.add,
             )
-            nc.vector.tensor_tensor(out=square[:, 0, :, 0:VECTOR_TOKENS, :], in0=offset[:], in1=offset[:], op=ALU.mult)
+            offsets[i] = offset
+
+        def square_offsets(i):
+            h_round = hidden_of_round(i)
+            square = act_pool.tile([P, 2, ROUND_PASSES, TOKENS, 2], F32)
+            nc.vector.tensor_tensor(
+                out=square[:, 0, :, 0:VECTOR_TOKENS, :], in0=offsets[i][:], in1=offsets[i][:], op=ALU.mult
+            )
             for e, first_token in ((1, 0), (0, VECTOR_TOKENS)):
                 nc.scalar.activation(
                     out=square[:, e, :, first_token:TOKENS, :],
@@ -294,6 +302,8 @@ def tile_kan1_pb_k_kernel(tc, h_mix, x, fc2_spline_w, fc2_base_w, fc2_base_b, ou
         y_ps = [y_pool.tile([P, TOKENS], F32, name="y_ps%d" % m) for m in range(OUT_TILES)]
 
         for step in range(-2, n_rounds + 2):
+            if is_spline(step + 2):
+                offsets_from_centre(step + 2)
             if is_spline(step - 1):
                 quantise_basis(step - 1)
             if is_round(step - 1):

@@ -1,5 +1,7 @@
 from contextlib import ExitStack
 
+import math
+
 import concourse.mybir as mybir
 from concourse.masks import make_identity
 
@@ -41,7 +43,7 @@ PARKED_CHUNKS = 3
 WEIGHTS_AHEAD = 3
 VECTOR_TOKENS = 448
 
-INV_D = 3.5
+SQUARE_SCALE = 3.5 / math.sqrt(7.0)
 
 FLOPS = 2 * TOKENS * 512 * (HIDDEN * CENTRES + HIDDEN)
 
@@ -78,7 +80,6 @@ def tile_kan1_pb_k_kernel(tc, h_mix, x, fc2_spline_w, fc2_base_w, fc2_base_b, ou
         h_t_pool = stack.enter_context(tc.tile_pool(name="h_t", bufs=CHUNKS))
         h_rep_pool = stack.enter_context(tc.tile_pool(name="h_rep", bufs=PARKED_CHUNKS))
         act_pool = stack.enter_context(tc.tile_pool(name="act", bufs=2))
-        offset_pool = stack.enter_context(tc.tile_pool(name="offset", bufs=2))
         act_mx_pool = stack.enter_context(tc.tile_pool(name="act_mx", bufs=2))
         res_pool = stack.enter_context(tc.tile_pool(name="res", bufs=OUT_TILES))
         y_pool = stack.enter_context(tc.psum_pool(name="y", bufs=1))
@@ -94,8 +95,17 @@ def tile_kan1_pb_k_kernel(tc, h_mix, x, fc2_spline_w, fc2_base_w, fc2_base_b, ou
         minus_centre = keep.tile([P, 2], F32)
         for e in range(2):
             nc.vector.tensor_scalar(
-                out=minus_centre[:, e : e + 1], in0=part_mod_f[:], scalar1=-2.0, scalar2=3.5 - e, op0=ALU.mult, op1=ALU.add
+                out=minus_centre[:, e : e + 1],
+                in0=part_mod_f[:],
+                scalar1=-2.0 / math.sqrt(7.0),
+                scalar2=(3.5 - e) / math.sqrt(7.0),
+                op0=ALU.mult,
+                op1=ALU.add,
             )
+        step_const = keep.tile([P, 1], F32)
+        nc.vector.tensor_scalar(
+            out=step_const[:], in0=part_mod_f[:], scalar1=-4.0 / 7.0, scalar2=6.0 / 7.0, op0=ALU.mult, op1=ALU.add
+        )
         ident_bf = keep.tile([P, P], BF16)
         make_identity(nc, ident_bf[:])
         ident_f32 = keep.tile([P, P], F32)
@@ -151,7 +161,6 @@ def tile_kan1_pb_k_kernel(tc, h_mix, x, fc2_spline_w, fc2_base_w, fc2_base_b, ou
         w_turned = {}
         w_grouped = {}
         w_mx = {}
-        offsets = {}
         squares = {}
         basis = {}
         moving = {}
@@ -199,38 +208,34 @@ def tile_kan1_pb_k_kernel(tc, h_mix, x, fc2_spline_w, fc2_base_w, fc2_base_b, ou
             first = ROUND_GROUPS * (r % CHUNK_ROUNDS)
             return h_rep[r // CHUNK_ROUNDS][:, first : first + ROUND_GROUPS, :].rearrange("q (a u) n -> q a n u", u=2)
 
-        def offsets_from_centre(i):
-            offset = offset_pool.tile([P, ROUND_PASSES, VECTOR_TOKENS, 2], F32)
-            nc.gpsimd.tensor_scalar(
-                out=offset[:],
-                in0=hidden_of_round(i)[:, :, 0:VECTOR_TOKENS, :],
-                scalar1=INV_D,
-                scalar2=minus_centre[:, 0:1],
-                op0=ALU.mult,
-                op1=ALU.add,
-            )
-            offsets[i] = offset
-
-        def square_offsets(i):
+        def square_on_scalar(i):
             h_round = hidden_of_round(i)
             square = act_pool.tile([P, 2, ROUND_PASSES, TOKENS, 2], F32)
-            nc.vector.tensor_tensor(
-                out=square[:, 0, :, 0:VECTOR_TOKENS, :], in0=offsets[i][:], in1=offsets[i][:], op=ALU.mult
-            )
             for e, first_token in ((1, 0), (0, VECTOR_TOKENS)):
                 nc.scalar.activation(
                     out=square[:, e, :, first_token:TOKENS, :],
                     in_=h_round[:, :, first_token:TOKENS, :],
                     func=ACT.Square,
-                    scale=INV_D,
+                    scale=SQUARE_SCALE,
                     bias=minus_centre[:, e : e + 1],
                 )
             squares[i] = square
 
+        def derive_on_vector(i):
+            for a in range(ROUND_PASSES):
+                nc.vector.scalar_tensor_tensor(
+                    out=squares[i][:, 0, a, 0:VECTOR_TOKENS, :],
+                    in0=hidden_of_round(i)[:, a, 0:VECTOR_TOKENS, :],
+                    scalar=step_const[:],
+                    in1=squares[i][:, 1, a, 0:VECTOR_TOKENS, :],
+                    op0=ALU.add,
+                    op1=ALU.add,
+                )
+
         def exponentials(i):
             basis_bf = act_pool.tile([P, ROUND_PASSES * TOKENS * 2, 2], BF16, align_bytes=64)
             nc.scalar.activation(
-                out=basis_bf[:], in_=squares[i][:].rearrange("q e a n u -> q (a n u) e"), func=ACT.Exp, scale=-1.0
+                out=basis_bf[:], in_=squares[i][:].rearrange("q e a n u -> q (a n u) e"), func=ACT.Exp, scale=-7.0
             )
             basis[i] = basis_bf
 
@@ -302,23 +307,23 @@ def tile_kan1_pb_k_kernel(tc, h_mix, x, fc2_spline_w, fc2_base_w, fc2_base_b, ou
         y_ps = [y_pool.tile([P, TOKENS], F32, name="y_ps%d" % m) for m in range(OUT_TILES)]
 
         for step in range(-2, n_rounds + 2):
-            if is_spline(step + 2):
-                offsets_from_centre(step + 2)
             if is_spline(step - 1):
                 quantise_basis(step - 1)
             if is_round(step - 1):
                 multiply(step - 1)
             if is_spline(step + 1):
-                square_offsets(step + 1)
+                square_on_scalar(step + 1)
+            if is_spline(step):
+                exponentials(step)
+            if is_round(step + 1):
+                group_weights(step + 1)
+            if is_spline(step + 1):
+                derive_on_vector(step + 1)
                 r = order[step + 1][1]
                 refill = r // CHUNK_ROUNDS + PARKED_CHUNKS
                 if r % CHUNK_ROUNDS == CHUNK_ROUNDS - 1 and refill < CHUNKS:
                     park_hidden(refill)
                     replicate_hidden(refill)
-            if is_spline(step):
-                exponentials(step)
-            if is_round(step + 1):
-                group_weights(step + 1)
             if is_round(step + 2):
                 turn_weights(step + 2)
                 if is_round(step + 2 + WEIGHTS_AHEAD):

@@ -39,9 +39,13 @@ CHUNK_GROUPS = CHUNK_HIDDEN // GROUP_HIDDEN
 ROUND_GROUPS = 2 * ROUND_PASSES
 CHUNK_ROUNDS = CHUNK_GROUPS // ROUND_GROUPS
 CHUNKS = HIDDEN // CHUNK_HIDDEN
-PARKED_CHUNKS = 3
+PARK_SLOTS = 2
+REPLICAS = 3
 WEIGHTS_AHEAD = 3
-VECTOR_TOKENS = 448
+TENSOR_TOKENS = 224
+BANK_TOKENS = 112
+TOKEN_BLOCKS = TENSOR_TOKENS // BANK_TOKENS
+ENGINE_TOKENS = TOKENS - TENSOR_TOKENS
 
 SQUARE_SCALE = 3.5 / math.sqrt(7.0)
 
@@ -59,11 +63,9 @@ def tile_kan1_pb_k_kernel(tc, h_mix, x, fc2_spline_w, fc2_base_w, fc2_base_b, ou
     out_rows = out.flatten_outer_dims()
     out_tiles = out_rows.rearrange("(g r) c -> r g c", r=P)
 
-    order = []
+    order = [("base", r) for r in range(BASE_ROUNDS)]
     for r in range(SPLINE_ROUNDS):
         order.append(("spline", r))
-        if r % 8 == 1:
-            order.append(("base", r // 8))
     n_rounds = len(order)
 
     def is_round(i):
@@ -78,8 +80,10 @@ def tile_kan1_pb_k_kernel(tc, h_mix, x, fc2_spline_w, fc2_base_w, fc2_base_b, ou
         w_pool = stack.enter_context(tc.tile_pool(name="w", bufs=2))
         w_mx_pool = stack.enter_context(tc.tile_pool(name="w_mx", bufs=3))
         h_t_pool = stack.enter_context(tc.tile_pool(name="h_t", bufs=CHUNKS))
-        h_rep_pool = stack.enter_context(tc.tile_pool(name="h_rep", bufs=PARKED_CHUNKS))
+        kinds_pool = stack.enter_context(tc.tile_pool(name="kinds", bufs=CHUNKS))
+        h_rep_pool = stack.enter_context(tc.tile_pool(name="h_rep", bufs=REPLICAS))
         act_pool = stack.enter_context(tc.tile_pool(name="act", bufs=2))
+        square_pool = stack.enter_context(tc.tile_pool(name="square", bufs=2))
         act_mx_pool = stack.enter_context(tc.tile_pool(name="act_mx", bufs=2))
         res_pool = stack.enter_context(tc.tile_pool(name="res", bufs=OUT_TILES))
         y_pool = stack.enter_context(tc.psum_pool(name="y", bufs=1))
@@ -111,19 +115,58 @@ def tile_kan1_pb_k_kernel(tc, h_mix, x, fc2_spline_w, fc2_base_w, fc2_base_b, ou
         ident_f32 = keep.tile([P, P], F32)
         make_identity(nc, ident_f32[:])
 
+        twice_place = keep.tile([P, GROUP_HIDDEN, COPIES], F32)
+        nc.gpsimd.iota(
+            twice_place[:],
+            pattern=[[0, GROUP_HIDDEN], [2, COPIES]],
+            base=0,
+            channel_multiplier=0,
+            allow_small_or_imprecise_dtypes=True,
+        )
+        centre_w = []
+        for e in range(2):
+            weights = keep.tile([P, GROUP_HIDDEN, COPIES], BF16, name="centre_w%d" % e)
+            seven_c = keep.tile([P, GROUP_HIDDEN, COPIES], F32, name="seven_c%d" % e)
+            nc.vector.tensor_scalar(
+                out=seven_c[:], in0=twice_place[:], scalar1=e - 3.5, scalar2=7.0, op0=ALU.add, op1=ALU.mult
+            )
+            for kind in range(3):
+                rows = slice(kind * GROUP_HIDDEN, (kind + 1) * GROUP_HIDDEN)
+                unit = ident_bf[rows, rows].unsqueeze(2).to_broadcast([GROUP_HIDDEN, GROUP_HIDDEN, COPIES])
+                if kind == 0:
+                    nc.vector.tensor_tensor(out=weights[rows], in0=seven_c[rows], in1=unit, op=ALU.mult)
+                else:
+                    nc.vector.tensor_scalar(
+                        out=weights[rows], in0=unit, scalar1=-12.25, scalar2=0.0, op0=ALU.mult, op1=ALU.add
+                    )
+            nc.vector.memset(weights[3 * GROUP_HIDDEN : P], 0.0)
+            ones_row = slice(3 * GROUP_HIDDEN, 3 * GROUP_HIDDEN + 1)
+            nc.vector.scalar_tensor_tensor(
+                out=weights[ones_row],
+                in0=seven_c[ones_row],
+                scalar=-1.0 / 49.0,
+                in1=seven_c[ones_row],
+                op0=ALU.mult,
+                op1=ALU.mult,
+            )
+            centre_w.append(weights)
+        h_rows_tiles = []
+        for n in range(REPLICAS):
+            rows_tile = keep.tile([P, CHUNK_GROUPS, TENSOR_TOKENS], BF16, name="h_rows%d" % n)
+            nc.gpsimd.memset(rows_tile[3 * GROUP_HIDDEN : P], 1.0)
+            h_rows_tiles.append(rows_tile)
+
         h_sb = []
-        for quarter in range(BASE_PASSES):
+
+        def load_hidden(quarter):
             h_quarter = keep.tile([P, TOKEN_TILES, K_PASS], BF16, name="h_quarter%d" % quarter)
             cols = slice(quarter * K_PASS, (quarter + 1) * K_PASS)
             nc.sync.dma_start(out=h_quarter[:], in_=h_rows[:, cols].rearrange("(t r) j -> r t j", r=P))
             h_sb.append(h_quarter)
-        x_sb = keep.tile([P, 2 * OUT_TILES, CHANNELS], BF16)
-        nc.gpsimd.dma_start(out=x_sb[:], in_=x_rows)
-        bias_rows = keep.tile([P, P], BF16)
-        nc.vector.memset(bias_rows[:], 0.0)
-        nc.gpsimd.dma_start(out=bias_rows[0:OUT_TILES, :], in_=fc2_base_b.rearrange("(m r) -> m r", r=P))
+
 
         h_t = {}
+        h_kinds = {}
         h_rep = {}
 
         def turn_hidden(chunk):
@@ -139,21 +182,44 @@ def tile_kan1_pb_k_kernel(tc, h_mix, x, fc2_spline_w, fc2_base_w, fc2_base_b, ou
             nc.vector.tensor_copy(out=turned[:], in_=h_t_ps[:])
             h_t[chunk] = turned
 
-        def parked_rows(chunk):
-            first_row = (chunk % PARKED_CHUNKS) * CHUNK_HIDDEN
-            return out_rows[first_row : first_row + CHUNK_HIDDEN, :]
+        def split_squares(chunk):
+            square = square_pool.tile([P, 2, TENSOR_TOKENS], F32)
+            nc.scalar.activation(out=square[:], in_=h_t[chunk][:, :, 0:TENSOR_TOKENS], func=ACT.Square)
+            kinds = kinds_pool.tile([P, 2, 2, TENSOR_TOKENS], BF16)
+            nc.gpsimd.tensor_scalar(
+                out=kinds[:, :, 0, :], in0=square[:], scalar1=1.0, scalar2=0.0, op0=ALU.mult, op1=ALU.add
+            )
+            nc.gpsimd.tensor_tensor(out=kinds[:, :, 1, :], in0=square[:], in1=kinds[:, :, 0, :], op=ALU.subtract)
+            h_kinds[chunk] = kinds
+
+        def parked_rows(chunk, kind, words):
+            first_row = (2 * (chunk % PARK_SLOTS) + (kind > 0)) * CHUNK_HIDDEN
+            return out_rows[first_row : first_row + CHUNK_HIDDEN, words]
 
         def park_hidden(chunk):
             nc.sync.dma_start(
-                out=parked_rows(chunk).rearrange("(a r) w -> r a w", r=P), in_=h_t[chunk][:].bitcast(F32)
+                out=parked_rows(chunk, 0, slice(0, TOKENS // 2)).rearrange("(a r) w -> r a w", r=P),
+                in_=h_t[chunk][:].bitcast(F32),
+            )
+            nc.sync.dma_start(
+                out=parked_rows(chunk, 1, slice(0, TENSOR_TOKENS)).rearrange("(a r) w -> r a w", r=P),
+                in_=h_kinds[chunk][:].rearrange("r a k n -> r a (k n)").bitcast(F32),
             )
 
         def replicate_hidden(chunk):
-            replicated = h_rep_pool.tile([P, CHUNK_GROUPS, TOKENS], BF16)
+            half = TENSOR_TOKENS // 2
+            for kind, first_word in enumerate((0, 0, half)):
+                nc.sync.dma_start(
+                    out=h_rows_tiles[chunk % REPLICAS][kind * GROUP_HIDDEN : (kind + 1) * GROUP_HIDDEN].bitcast(F32),
+                    in_=parked_rows(chunk, kind, slice(first_word, first_word + half)).rearrange(
+                        "(a r) w -> r a w", r=GROUP_HIDDEN
+                    ),
+                )
+            replicated = h_rep_pool.tile([P, CHUNK_GROUPS, ENGINE_TOKENS], BF16)
             for copy in range(COPIES):
                 nc.sync.dma_start(
                     out=replicated[copy:P:COPIES, :, :].bitcast(F32),
-                    in_=parked_rows(chunk).rearrange("(a r) w -> r a w", r=GROUP_HIDDEN),
+                    in_=parked_rows(chunk, 0, slice(half, TOKENS // 2)).rearrange("(a r) w -> r a w", r=GROUP_HIDDEN),
                 )
             h_rep[chunk] = replicated
 
@@ -161,6 +227,7 @@ def tile_kan1_pb_k_kernel(tc, h_mix, x, fc2_spline_w, fc2_base_w, fc2_base_b, ou
         w_turned = {}
         w_grouped = {}
         w_mx = {}
+        exponents = {}
         squares = {}
         basis = {}
         moving = {}
@@ -208,53 +275,90 @@ def tile_kan1_pb_k_kernel(tc, h_mix, x, fc2_spline_w, fc2_base_w, fc2_base_b, ou
             first = ROUND_GROUPS * (r % CHUNK_ROUNDS)
             return h_rep[r // CHUNK_ROUNDS][:, first : first + ROUND_GROUPS, :].rearrange("q (a u) n -> q a n u", u=2)
 
+        def exponents_on_tensor(i):
+            r = order[i][1]
+            rows_tile = h_rows_tiles[(r // CHUNK_ROUNDS) % REPLICAS]
+            banks = []
+            for a in range(ROUND_PASSES):
+                for block in range(TOKEN_BLOCKS):
+                    bank = turn_pool.tile([P, 2, 2, P], F32, tag="turn")
+                    tokens = slice(block * BANK_TOKENS, (block + 1) * BANK_TOKENS)
+                    for e in range(2):
+                        for u in range(2):
+                            group = ROUND_GROUPS * (r % CHUNK_ROUNDS) + 2 * a + u
+                            nc.tensor.matmul(
+                                bank[:, u, e, 0:BANK_TOKENS],
+                                lhsT=centre_w[e][:].rearrange("r j i -> r (j i)"),
+                                rhs=rows_tile[:, group, tokens],
+                                start=True,
+                                stop=True,
+                            )
+                    banks.append(bank)
+            exponents[i] = banks
+
         def square_on_scalar(i):
-            h_round = hidden_of_round(i)
-            square = act_pool.tile([P, 2, ROUND_PASSES, TOKENS, 2], F32)
-            for e, first_token in ((1, 0), (0, VECTOR_TOKENS)):
-                nc.scalar.activation(
-                    out=square[:, e, :, first_token:TOKENS, :],
-                    in_=h_round[:, :, first_token:TOKENS, :],
-                    func=ACT.Square,
-                    scale=SQUARE_SCALE,
-                    bias=minus_centre[:, e : e + 1],
-                )
+            square = act_pool.tile([P, 2, ROUND_PASSES, ENGINE_TOKENS, 2], F32)
+            nc.scalar.activation(
+                out=square[:, 1],
+                in_=hidden_of_round(i),
+                func=ACT.Square,
+                scale=SQUARE_SCALE,
+                bias=minus_centre[:, 1:2],
+            )
             squares[i] = square
 
         def derive_on_vector(i):
             for a in range(ROUND_PASSES):
                 nc.vector.scalar_tensor_tensor(
-                    out=squares[i][:, 0, a, 0:VECTOR_TOKENS, :],
-                    in0=hidden_of_round(i)[:, a, 0:VECTOR_TOKENS, :],
+                    out=squares[i][:, 0, a],
+                    in0=hidden_of_round(i)[:, a],
                     scalar=step_const[:],
-                    in1=squares[i][:, 1, a, 0:VECTOR_TOKENS, :],
+                    in1=squares[i][:, 1, a],
                     op0=ALU.add,
                     op1=ALU.add,
                 )
 
-        def exponentials(i):
-            basis_bf = act_pool.tile([P, ROUND_PASSES * TOKENS * 2, 2], BF16, align_bytes=64)
-            nc.scalar.activation(
-                out=basis_bf[:], in_=squares[i][:].rearrange("q e a n u -> q (a n u) e"), func=ACT.Exp, scale=-7.0
-            )
-            basis[i] = basis_bf
+        def exponentials_of_tensor(i, passes):
+            if i not in basis:
+                basis_bf = act_pool.tile([P, ROUND_PASSES, TOKENS, PACK], BF16, align_bytes=64)
+                basis[i] = basis_bf
+            for a in passes:
+                for block in range(TOKEN_BLOCKS):
+                    nc.scalar.activation(
+                        out=basis[i][:, a, block * BANK_TOKENS : (block + 1) * BANK_TOKENS, :],
+                        in_=exponents[i][a * TOKEN_BLOCKS + block][:, :, :, 0:BANK_TOKENS].rearrange(
+                            "q u e n -> q n (u e)"
+                        ),
+                        func=ACT.Exp,
+                    )
 
-        def quantise_basis(i):
-            codes = act_mx_pool.tile([P, ROUND_PASSES, TOKENS], U32, align_bytes=64)
-            scales = act_mx_pool.tile([P, ROUND_PASSES, TOKENS], U8, align_bytes=64)
+        def exponentials_of_squares(i, passes):
+            a = slice(passes.start, passes.stop)
+            nc.scalar.activation(
+                out=basis[i][:, a, TENSOR_TOKENS:TOKENS, :].rearrange("q a n (u e) -> q a (n u) e", e=2),
+                in_=squares[i][:, :, a].rearrange("q e a n u -> q a (n u) e"),
+                func=ACT.Exp,
+                scale=-7.0,
+            )
+
+        def quantise_basis(i, passes):
+            if i not in moving:
+                codes = act_mx_pool.tile([P, ROUND_PASSES, TOKENS], U32, align_bytes=64)
+                scales = act_mx_pool.tile([P, ROUND_PASSES, TOKENS], U8, align_bytes=64)
+                moving[i] = (codes[:], scales[:])
+            a = slice(passes.start, passes.stop)
             quantise(
                 nc,
-                codes[:].rearrange("q a n -> q (a n)"),
-                scales[:].rearrange("q a n -> q (a n)"),
-                basis[i][:].rearrange("q n e -> q (n e)"),
+                moving[i][0][:, a].rearrange("q a n -> q (a n)"),
+                moving[i][1][:, a].rearrange("q a n -> q (a n)"),
+                basis[i][:, a].rearrange("q a n t -> q (a n t)"),
             )
-            moving[i] = (codes[:], scales[:])
 
-        def multiply(i):
+        def multiply(i, passes):
             w_codes, w_scales = w_mx[i]
             codes, scales = moving[i]
             for m in range(OUT_TILES):
-                for a in range(ROUND_PASSES):
+                for a in passes:
                     cols = slice((a * OUT_TILES + m) * P, (a * OUT_TILES + m + 1) * P)
                     nc.tensor.matmul_mx(
                         out=y_ps[m][:],
@@ -268,7 +372,9 @@ def tile_kan1_pb_k_kernel(tc, h_mix, x, fc2_spline_w, fc2_base_w, fc2_base_b, ou
 
         silu_codes = keep.tile([P, BASE_PASSES, TOKENS], U32, align_bytes=64)
         silu_scales = keep.tile([P, BASE_PASSES, TOKENS], U8, align_bytes=64)
-        for g in range(BASE_PASSES):
+        silu = {}
+
+        def make_silu(g):
             silu_bf = act_pool.tile([P, TOKENS, PACK], BF16, align_bytes=64)
             for half in range(2):
                 h_w_ps = turn_pool.tile([P, 2, 2 * P], F32, tag="turn")
@@ -284,52 +390,97 @@ def tile_kan1_pb_k_kernel(tc, h_mix, x, fc2_spline_w, fc2_base_w, fc2_base_b, ou
                     in_=h_w_ps[:].bitcast(BF16).rearrange("q u (n e) -> q n u e", e=2),
                     func=ACT.Silu,
                 )
-            turn_hidden(2 * g)
-            turn_hidden(2 * g + 1)
-            quantise(nc, silu_codes[:, g, :], silu_scales[:, g, :], silu_bf[:].rearrange("q n t -> q (n t)"))
+            silu[g] = silu_bf
+
+        def quantise_silu(g):
+            quantise(nc, silu_codes[:, g, :], silu_scales[:, g, :], silu[g][:].rearrange("q n t -> q (n t)"))
 
         for b in range(BASE_ROUNDS):
             passes = slice(b * ROUND_PASSES, (b + 1) * ROUND_PASSES)
             moving[order.index(("base", b))] = (silu_codes[:, passes, :], silu_scales[:, passes, :])
 
-        for chunk in range(PARKED_CHUNKS):
-            park_hidden(chunk)
-            load_weights(chunk)
-            replicate_hidden(chunk)
-        for i in range(PARKED_CHUNKS, WEIGHTS_AHEAD):
-            load_weights(i)
-
-        bias_ps = turn_pool.tile([P, P], BF16, tag="turn")
-        nc.tensor.transpose(bias_ps[:], bias_rows[:], ident_bf[:])
-        bias_col = keep.tile([P, OUT_TILES], F32)
-        nc.vector.tensor_copy(out=bias_col[:], in_=bias_ps[:, 0:OUT_TILES])
+        load_hidden(0)
+        load_weights(0)
+        load_hidden(1)
+        load_weights(1)
+        load_hidden(2)
+        load_hidden(3)
+        turn_hidden(0)
+        split_squares(0)
+        park_hidden(0)
+        turn_hidden(1)
+        make_silu(0)
+        turn_weights(0)
+        split_squares(1)
+        park_hidden(1)
+        replicate_hidden(0)
+        load_weights(2)
+        replicate_hidden(1)
+        group_weights(0)
+        quantise_silu(0)
+        make_silu(1)
+        quantise_weights(0)
+        turn_weights(1)
+        load_weights(3)
+        make_silu(2)
+        quantise_silu(1)
+        group_weights(1)
+        make_silu(3)
+        load_weights(4)
 
         y_ps = [y_pool.tile([P, TOKENS], F32, name="y_ps%d" % m) for m in range(OUT_TILES)]
 
-        for step in range(-2, n_rounds + 2):
-            if is_spline(step - 1):
-                quantise_basis(step - 1)
-            if is_round(step - 1):
-                multiply(step - 1)
-            if is_spline(step + 1):
-                square_on_scalar(step + 1)
+        both = range(ROUND_PASSES)
+        for step in range(1, n_rounds + 1):
+            last = step >= n_rounds - 1
+            parts = [range(a, a + 1) for a in both] if last else [both]
             if is_spline(step):
-                exponentials(step)
+                for part in parts:
+                    exponentials_of_tensor(step, part)
+                    if last:
+                        exponentials_of_squares(step, part)
+            if is_round(step + 1):
+                turn_weights(step + 1)
+                if is_round(step + 1 + WEIGHTS_AHEAD):
+                    load_weights(step + 1 + WEIGHTS_AHEAD)
+            if is_spline(step - 1):
+                for part in parts if step == n_rounds else [both]:
+                    quantise_basis(step - 1, part)
+                    if step == n_rounds:
+                        multiply(step - 1, part)
+            if step < n_rounds:
+                multiply(step - 1, both)
+                quantise_weights(step)
             if is_round(step + 1):
                 group_weights(step + 1)
+            if step == 1:
+                quantise_silu(2)
+                quantise_silu(3)
             if is_spline(step + 1):
+                ahead, odd = divmod(order[step + 1][1], CHUNK_ROUNDS)
+                if not odd and ahead + 2 < CHUNKS:
+                    turn_hidden(ahead + 2)
+                if step == n_rounds - 2:
+                    bias_ps = turn_pool.tile([P, P], BF16, tag="turn")
+                    nc.tensor.transpose(bias_ps[:], bias_rows[:], ident_bf[:])
+                    bias_col = keep.tile([P, OUT_TILES], F32)
+                    nc.vector.tensor_copy(out=bias_col[:], in_=bias_ps[:, 0:OUT_TILES])
+                exponents_on_tensor(step + 1)
+                square_on_scalar(step + 1)
                 derive_on_vector(step + 1)
-                r = order[step + 1][1]
-                refill = r // CHUNK_ROUNDS + PARKED_CHUNKS
-                if r % CHUNK_ROUNDS == CHUNK_ROUNDS - 1 and refill < CHUNKS:
-                    park_hidden(refill)
-                    replicate_hidden(refill)
-            if is_round(step + 2):
-                turn_weights(step + 2)
-                if is_round(step + 2 + WEIGHTS_AHEAD):
-                    load_weights(step + 2 + WEIGHTS_AHEAD)
-            if is_round(step):
-                quantise_weights(step)
+                if odd and ahead + 2 < CHUNKS:
+                    split_squares(ahead + 2)
+                    park_hidden(ahead + 2)
+                if not odd and 1 <= ahead and ahead + 1 < CHUNKS:
+                    replicate_hidden(ahead + 1)
+            if is_spline(step) and not last:
+                exponentials_of_squares(step, both)
+            if step == 4:
+                bias_rows = keep.tile([P, P], BF16)
+                nc.gpsimd.memset(bias_rows[:], 0.0)
+                nc.sync.dma_start(out=bias_rows[0:OUT_TILES, :], in_=fc2_base_b.rearrange("(m r) -> m r", r=P))
+                x_sb = keep.tile([P, 2 * OUT_TILES, CHANNELS], BF16)
+                nc.sync.dma_start(out=x_sb[:], in_=x_rows)
 
         for m in range(OUT_TILES):
             res = res_pool.tile([P, 2, CHANNELS], F32)

@@ -42,10 +42,11 @@ CHUNKS = HIDDEN // CHUNK_HIDDEN
 PARK_SLOTS = 2
 REPLICAS = 3
 WEIGHTS_AHEAD = 3
-TENSOR_TOKENS = 224
-BANK_TOKENS = 112
+TENSOR_TOKENS = 128
+BANK_TOKENS = 128
 TOKEN_BLOCKS = TENSOR_TOKENS // BANK_TOKENS
 ENGINE_TOKENS = TOKENS - TENSOR_TOKENS
+DERIVED_TOKENS = 320
 
 SQUARE_SCALE = 3.5 / math.sqrt(7.0)
 
@@ -74,6 +75,8 @@ def tile_kan1_pb_k_kernel(tc, h_mix, x, fc2_spline_w, fc2_base_w, fc2_base_b, ou
     def is_spline(i):
         return is_round(i) and order[i][0] == "spline"
 
+    both = range(ROUND_PASSES)
+
     with ExitStack() as stack:
         keep = stack.enter_context(tc.tile_pool(name="keep", bufs=1))
         w_raw_pool = stack.enter_context(tc.tile_pool(name="w_raw", bufs=WEIGHTS_AHEAD))
@@ -87,7 +90,7 @@ def tile_kan1_pb_k_kernel(tc, h_mix, x, fc2_spline_w, fc2_base_w, fc2_base_b, ou
         act_mx_pool = stack.enter_context(tc.tile_pool(name="act_mx", bufs=2))
         res_pool = stack.enter_context(tc.tile_pool(name="res", bufs=OUT_TILES))
         y_pool = stack.enter_context(tc.psum_pool(name="y", bufs=1))
-        turn_pool = stack.enter_context(tc.psum_pool(name="turn", bufs=4))
+        turn_pool = stack.enter_context(tc.psum_pool(name="turn", bufs=2))
         stack.enter_context(tc.manual_schedule())
 
         part_idx = keep.tile([P, 1], I32)
@@ -153,8 +156,12 @@ def tile_kan1_pb_k_kernel(tc, h_mix, x, fc2_spline_w, fc2_base_w, fc2_base_b, ou
         h_rows_tiles = []
         for n in range(REPLICAS):
             rows_tile = keep.tile([P, CHUNK_GROUPS, TENSOR_TOKENS], BF16, name="h_rows%d" % n)
-            nc.gpsimd.memset(rows_tile[3 * GROUP_HIDDEN : P], 1.0)
             h_rows_tiles.append(rows_tile)
+
+        def fill_ones(n):
+            nc.vector.memset(h_rows_tiles[n][3 * GROUP_HIDDEN : P], 1.0)
+
+        fill_ones(0)
 
         h_sb = []
 
@@ -165,6 +172,7 @@ def tile_kan1_pb_k_kernel(tc, h_mix, x, fc2_spline_w, fc2_base_w, fc2_base_b, ou
             h_sb.append(h_quarter)
 
 
+        h_turned = {}
         h_t = {}
         h_kinds = {}
         h_rep = {}
@@ -178,6 +186,10 @@ def tile_kan1_pb_k_kernel(tc, h_mix, x, fc2_spline_w, fc2_base_w, fc2_base_b, ou
                     nc.tensor.transpose(
                         h_t_ps[:, half, t * P : (t + 1) * P], h_sb[quarter][:, t, first : first + P], ident_bf[:]
                     )
+            h_turned[chunk] = h_t_ps
+
+        def keep_hidden(chunk):
+            h_t_ps = h_turned[chunk]
             turned = h_t_pool.tile([P, 2, TOKENS], BF16)
             nc.vector.tensor_copy(out=turned[:], in_=h_t_ps[:])
             h_t[chunk] = turned
@@ -241,28 +253,28 @@ def tile_kan1_pb_k_kernel(tc, h_mix, x, fc2_spline_w, fc2_base_w, fc2_base_b, ou
             )
             w_raw[i] = raw
 
-        def turn_weights(i):
-            banks = []
-            for a in range(ROUND_PASSES):
-                for half in range(2):
-                    w_t_ps = turn_pool.tile([P, 2, 2, P], F32, tag="turn")
-                    for m in range(2):
-                        for u in range(2):
-                            first = a * WORDS + u * P
-                            nc.tensor.transpose(
-                                w_t_ps[:, m, u, :],
-                                w_raw[i][:, 2 * half + m, :].bitcast(F32)[:, first : first + P],
-                                ident_f32[:],
-                            )
-                    banks.append(w_t_ps)
-            w_turned[i] = banks
+        def turn_weights(i, a):
+            for half in range(2):
+                w_t_ps = turn_pool.tile([P, 2, 2, P], F32, tag="turn")
+                for m in range(2):
+                    for u in range(2):
+                        first = a * WORDS + u * P
+                        nc.tensor.transpose(
+                            w_t_ps[:, m, u, :],
+                            w_raw[i][:, 2 * half + m, :].bitcast(F32)[:, first : first + P],
+                            ident_f32[:],
+                        )
+                w_turned[i, a, half] = w_t_ps
 
-        def group_weights(i):
-            w_bf = w_pool.tile([P, ROUND_PASSES * OUT_TILES * P * PACK], BF16, align_bytes=64)
-            w_words = w_bf[:].bitcast(F32).rearrange("q (b m r u) -> q b m r u", m=2, r=P, u=2)
-            for bank in range(2 * ROUND_PASSES):
-                nc.vector.tensor_copy(out=w_words[:, bank], in_=w_turned[i][bank][:].rearrange("q m u r -> q m r u"))
-            w_grouped[i] = w_bf
+        def group_weights(i, a):
+            if i not in w_grouped:
+                w_bf = w_pool.tile([P, ROUND_PASSES * OUT_TILES * P * PACK], BF16, align_bytes=64)
+                w_grouped[i] = w_bf
+            w_words = w_grouped[i][:].bitcast(F32).rearrange("q (b m r u) -> q b m r u", m=2, r=P, u=2)
+            for half in range(2):
+                nc.vector.tensor_copy(
+                    out=w_words[:, 2 * a + half], in_=w_turned[i, a, half][:].rearrange("q m u r -> q m r u")
+                )
 
         def quantise_weights(i):
             w_codes = w_mx_pool.tile([P, ROUND_PASSES * OUT_TILES * P], U32, align_bytes=64)
@@ -275,62 +287,58 @@ def tile_kan1_pb_k_kernel(tc, h_mix, x, fc2_spline_w, fc2_base_w, fc2_base_b, ou
             first = ROUND_GROUPS * (r % CHUNK_ROUNDS)
             return h_rep[r // CHUNK_ROUNDS][:, first : first + ROUND_GROUPS, :].rearrange("q (a u) n -> q a n u", u=2)
 
-        def exponents_on_tensor(i):
+        def exponents_on_tensor(i, a):
             r = order[i][1]
             rows_tile = h_rows_tiles[(r // CHUNK_ROUNDS) % REPLICAS]
-            banks = []
-            for a in range(ROUND_PASSES):
-                for block in range(TOKEN_BLOCKS):
-                    bank = turn_pool.tile([P, 2, 2, P], F32, tag="turn")
-                    tokens = slice(block * BANK_TOKENS, (block + 1) * BANK_TOKENS)
-                    for e in range(2):
-                        for u in range(2):
-                            group = ROUND_GROUPS * (r % CHUNK_ROUNDS) + 2 * a + u
-                            nc.tensor.matmul(
-                                bank[:, u, e, 0:BANK_TOKENS],
-                                lhsT=centre_w[e][:].rearrange("r j i -> r (j i)"),
-                                rhs=rows_tile[:, group, tokens],
-                                start=True,
-                                stop=True,
-                            )
-                    banks.append(bank)
-            exponents[i] = banks
+            for block in range(TOKEN_BLOCKS):
+                bank = turn_pool.tile([P, 2, 2, P], F32, tag="exponents")
+                tokens = slice(block * BANK_TOKENS, (block + 1) * BANK_TOKENS)
+                for e in range(2):
+                    for u in range(2):
+                        group = ROUND_GROUPS * (r % CHUNK_ROUNDS) + 2 * a + u
+                        nc.tensor.matmul(
+                            bank[:, u, e, 0:BANK_TOKENS],
+                            lhsT=centre_w[e][:].rearrange("r j i -> r (j i)"),
+                            rhs=rows_tile[:, group, tokens],
+                            start=True,
+                            stop=True,
+                        )
+                exponents[i, a, block] = bank
 
         def square_on_scalar(i):
             square = act_pool.tile([P, 2, ROUND_PASSES, ENGINE_TOKENS, 2], F32)
-            nc.scalar.activation(
-                out=square[:, 1],
-                in_=hidden_of_round(i),
-                func=ACT.Square,
-                scale=SQUARE_SCALE,
-                bias=minus_centre[:, 1:2],
-            )
+            for e, first_token in ((1, 0), (0, DERIVED_TOKENS)):
+                if first_token < ENGINE_TOKENS:
+                    nc.scalar.activation(
+                        out=square[:, e, :, first_token:ENGINE_TOKENS, :],
+                        in_=hidden_of_round(i)[:, :, first_token:ENGINE_TOKENS, :],
+                        func=ACT.Square,
+                        scale=SQUARE_SCALE,
+                        bias=minus_centre[:, e : e + 1],
+                    )
             squares[i] = square
 
         def derive_on_vector(i):
             for a in range(ROUND_PASSES):
                 nc.vector.scalar_tensor_tensor(
-                    out=squares[i][:, 0, a],
-                    in0=hidden_of_round(i)[:, a],
+                    out=squares[i][:, 0, a, 0:DERIVED_TOKENS, :],
+                    in0=hidden_of_round(i)[:, a, 0:DERIVED_TOKENS, :],
                     scalar=step_const[:],
-                    in1=squares[i][:, 1, a],
+                    in1=squares[i][:, 1, a, 0:DERIVED_TOKENS, :],
                     op0=ALU.add,
                     op1=ALU.add,
                 )
 
-        def exponentials_of_tensor(i, passes):
+        def exponentials_of_tensor(i, a):
             if i not in basis:
                 basis_bf = act_pool.tile([P, ROUND_PASSES, TOKENS, PACK], BF16, align_bytes=64)
                 basis[i] = basis_bf
-            for a in passes:
-                for block in range(TOKEN_BLOCKS):
-                    nc.scalar.activation(
-                        out=basis[i][:, a, block * BANK_TOKENS : (block + 1) * BANK_TOKENS, :],
-                        in_=exponents[i][a * TOKEN_BLOCKS + block][:, :, :, 0:BANK_TOKENS].rearrange(
-                            "q u e n -> q n (u e)"
-                        ),
-                        func=ACT.Exp,
-                    )
+            for block in range(TOKEN_BLOCKS):
+                nc.scalar.activation(
+                    out=basis[i][:, a, block * BANK_TOKENS : (block + 1) * BANK_TOKENS, :],
+                    in_=exponents[i, a, block][:, :, :, 0:BANK_TOKENS].rearrange("q u e n -> q n (u e)"),
+                    func=ACT.Exp,
+                )
 
         def exponentials_of_squares(i, passes):
             a = slice(passes.start, passes.stop)
@@ -354,10 +362,10 @@ def tile_kan1_pb_k_kernel(tc, h_mix, x, fc2_spline_w, fc2_base_w, fc2_base_b, ou
                 basis[i][:, a].rearrange("q a n t -> q (a n t)"),
             )
 
-        def multiply(i, passes):
+        def multiply(i, tiles, passes):
             w_codes, w_scales = w_mx[i]
             codes, scales = moving[i]
-            for m in range(OUT_TILES):
+            for m in tiles:
                 for a in passes:
                     cols = slice((a * OUT_TILES + m) * P, (a * OUT_TILES + m + 1) * P)
                     nc.tensor.matmul_mx(
@@ -377,7 +385,7 @@ def tile_kan1_pb_k_kernel(tc, h_mix, x, fc2_spline_w, fc2_base_w, fc2_base_b, ou
         def make_silu(g):
             silu_bf = act_pool.tile([P, TOKENS, PACK], BF16, align_bytes=64)
             for half in range(2):
-                h_w_ps = turn_pool.tile([P, 2, 2 * P], F32, tag="turn")
+                h_w_ps = turn_pool.tile([P, 2, 2 * P], F32, tag="exponents")
                 for u in range(2):
                     for t in range(2):
                         nc.tensor.transpose(
@@ -405,75 +413,93 @@ def tile_kan1_pb_k_kernel(tc, h_mix, x, fc2_spline_w, fc2_base_w, fc2_base_b, ou
         load_weights(1)
         load_hidden(2)
         load_hidden(3)
-        turn_hidden(0)
-        split_squares(0)
-        park_hidden(0)
-        turn_hidden(1)
+        y_ps = [y_pool.tile([P, TOKENS], F32, name="y_ps%d" % m) for m in range(OUT_TILES)]
+
+        for chunk in range(2):
+            turn_hidden(chunk)
+            keep_hidden(chunk)
+            split_squares(chunk)
+            park_hidden(chunk)
+            if chunk == 0:
+                load_weights(2)
+        fill_ones(1)
+        fill_ones(2)
         make_silu(0)
-        turn_weights(0)
-        split_squares(1)
-        park_hidden(1)
         replicate_hidden(0)
-        load_weights(2)
         replicate_hidden(1)
-        group_weights(0)
+        for a in both:
+            turn_weights(0, a)
+            group_weights(0, a)
         quantise_silu(0)
         make_silu(1)
         quantise_weights(0)
-        turn_weights(1)
+        turn_weights(1, 0)
         load_weights(3)
         make_silu(2)
         quantise_silu(1)
-        group_weights(1)
+        group_weights(1, 0)
+        turn_weights(1, 1)
         make_silu(3)
+        group_weights(1, 1)
         load_weights(4)
+        turn_weights(2, 0)
+        quantise_weights(1)
+        quantise_silu(2)
+        group_weights(2, 0)
+        turn_weights(2, 1)
+        quantise_silu(3)
+        load_weights(5)
+        exponents_on_tensor(2, 0)
+        square_on_scalar(2)
+        exponentials_of_tensor(2, 0)
+        group_weights(2, 1)
+        turn_hidden(2)
+        keep_hidden(2)
+        exponents_on_tensor(2, 1)
+        exponentials_of_tensor(2, 1)
+        multiply(0, range(0, 2), both)
+        turn_weights(3, 0)
+        derive_on_vector(2)
+        exponentials_of_squares(2, both)
+        multiply(0, range(2, OUT_TILES), both)
 
-        y_ps = [y_pool.tile([P, TOKENS], F32, name="y_ps%d" % m) for m in range(OUT_TILES)]
-
-        both = range(ROUND_PASSES)
-        for step in range(1, n_rounds + 1):
-            last = step >= n_rounds - 1
-            parts = [range(a, a + 1) for a in both] if last else [both]
-            if is_spline(step):
-                for part in parts:
-                    exponentials_of_tensor(step, part)
-                    if last:
-                        exponentials_of_squares(step, part)
-            if is_round(step + 1):
-                turn_weights(step + 1)
-                if is_round(step + 1 + WEIGHTS_AHEAD):
-                    load_weights(step + 1 + WEIGHTS_AHEAD)
+        for step in range(2, n_rounds - 1):
+            if step > BASE_ROUNDS:
+                exponentials_of_tensor(step, 0)
+                exponents_on_tensor(step, 1)
             if is_spline(step - 1):
-                for part in parts if step == n_rounds else [both]:
-                    quantise_basis(step - 1, part)
-                    if step == n_rounds:
-                        multiply(step - 1, part)
-            if step < n_rounds:
-                multiply(step - 1, both)
-                quantise_weights(step)
-            if is_round(step + 1):
-                group_weights(step + 1)
-            if step == 1:
-                quantise_silu(2)
-                quantise_silu(3)
-            if is_spline(step + 1):
-                ahead, odd = divmod(order[step + 1][1], CHUNK_ROUNDS)
-                if not odd and ahead + 2 < CHUNKS:
-                    turn_hidden(ahead + 2)
-                if step == n_rounds - 2:
-                    bias_ps = turn_pool.tile([P, P], BF16, tag="turn")
-                    nc.tensor.transpose(bias_ps[:], bias_rows[:], ident_bf[:])
-                    bias_col = keep.tile([P, OUT_TILES], F32)
-                    nc.vector.tensor_copy(out=bias_col[:], in_=bias_ps[:, 0:OUT_TILES])
-                exponents_on_tensor(step + 1)
-                square_on_scalar(step + 1)
-                derive_on_vector(step + 1)
-                if odd and ahead + 2 < CHUNKS:
-                    split_squares(ahead + 2)
-                    park_hidden(ahead + 2)
-                if not odd and 1 <= ahead and ahead + 1 < CHUNKS:
-                    replicate_hidden(ahead + 1)
-            if is_spline(step) and not last:
+                quantise_basis(step - 1, both)
+            multiply(step - 1, range(0, 1), both)
+            group_weights(step + 1, 0)
+            turn_weights(step + 1, 1)
+            if is_round(step + 1 + WEIGHTS_AHEAD):
+                load_weights(step + 1 + WEIGHTS_AHEAD)
+            multiply(step - 1, range(1, OUT_TILES), both)
+            square_on_scalar(step + 1)
+            if step > BASE_ROUNDS:
+                exponentials_of_tensor(step, 1)
+            quantise_weights(step)
+            group_weights(step + 1, 1)
+            exponents_on_tensor(step + 1, 0)
+            ahead, odd = divmod(order[step + 1][1], CHUNK_ROUNDS)
+            if not odd and ahead + 2 < CHUNKS:
+                turn_hidden(ahead + 2)
+            if step == n_rounds - 2:
+                bias_ps = turn_pool.tile([P, P], BF16, tag="turn")
+                nc.tensor.transpose(bias_ps[:], bias_rows[:], ident_bf[:])
+                bias_col = keep.tile([P, OUT_TILES], F32)
+                nc.vector.tensor_copy(out=bias_col[:], in_=bias_ps[:, 0:OUT_TILES])
+            derive_on_vector(step + 1)
+            if not odd and ahead + 2 < CHUNKS:
+                keep_hidden(ahead + 2)
+            if odd and ahead + 2 < CHUNKS:
+                split_squares(ahead + 2)
+                park_hidden(ahead + 2)
+            if not odd and 1 <= ahead and ahead + 1 < CHUNKS:
+                replicate_hidden(ahead + 1)
+            if is_round(step + 2):
+                turn_weights(step + 2, 0)
+            if step > BASE_ROUNDS:
                 exponentials_of_squares(step, both)
             if step == 4:
                 bias_rows = keep.tile([P, P], BF16)
@@ -481,6 +507,19 @@ def tile_kan1_pb_k_kernel(tc, h_mix, x, fc2_spline_w, fc2_base_w, fc2_base_b, ou
                 nc.sync.dma_start(out=bias_rows[0:OUT_TILES, :], in_=fc2_base_b.rearrange("(m r) -> m r", r=P))
                 x_sb = keep.tile([P, 2 * OUT_TILES, CHANNELS], BF16)
                 nc.sync.dma_start(out=x_sb[:], in_=x_rows)
+
+        final = n_rounds - 1
+        quantise_basis(final - 1, both)
+        quantise_weights(final)
+        for a in both:
+            one = range(a, a + 1)
+            exponentials_of_tensor(final, a)
+            if a == 0:
+                exponents_on_tensor(final, 1)
+                multiply(final - 1, range(OUT_TILES), both)
+            exponentials_of_squares(final, one)
+            quantise_basis(final, one)
+            multiply(final, range(OUT_TILES), one)
 
         for m in range(OUT_TILES):
             res = res_pool.tile([P, 2, CHANNELS], F32)

@@ -35,22 +35,26 @@ SPLINE_ROUNDS = HIDDEN * CENTRES // ROUND_K
 COPIES = 4
 GROUP_HIDDEN = P // COPIES
 CHUNK_HIDDEN = 2 * P
-CHUNK_GROUPS = CHUNK_HIDDEN // GROUP_HIDDEN
 ROUND_GROUPS = 2 * ROUND_PASSES
-CHUNK_ROUNDS = CHUNK_GROUPS // ROUND_GROUPS
+CHUNK_ROUNDS = CHUNK_HIDDEN // P
 CHUNKS = HIDDEN // CHUNK_HIDDEN
-PARK_SLOTS = 2
-REPLICAS = 3
+PARK_SLOTS = 4
+REPLICAS = 4
 WEIGHTS_AHEAD = 3
-TENSOR_TOKENS = 128
 BANK_TOKENS = 128
-TOKEN_BLOCKS = TENSOR_TOKENS // BANK_TOKENS
-ENGINE_TOKENS = TOKENS - TENSOR_TOKENS
-DERIVED_TOKENS = 320
+MAX_TENSOR_TOKENS = 2 * BANK_TOKENS
 
 SQUARE_SCALE = 3.5 / math.sqrt(7.0)
 
 FLOPS = 2 * TOKENS * 512 * (HIDDEN * CENTRES + HIDDEN)
+
+
+def tensor_tokens(r):
+    return BANK_TOKENS if r % 4 == 3 else 2 * BANK_TOKENS
+
+
+def derived_tokens(r):
+    return 320 if r % 4 == 3 else 256
 
 
 def quantise(nc, codes, scales, values):
@@ -82,8 +86,8 @@ def tile_kan1_pb_k_kernel(tc, h_mix, x, fc2_spline_w, fc2_base_w, fc2_base_b, ou
         w_raw_pool = stack.enter_context(tc.tile_pool(name="w_raw", bufs=WEIGHTS_AHEAD))
         w_pool = stack.enter_context(tc.tile_pool(name="w", bufs=2))
         w_mx_pool = stack.enter_context(tc.tile_pool(name="w_mx", bufs=3))
-        h_t_pool = stack.enter_context(tc.tile_pool(name="h_t", bufs=CHUNKS))
-        kinds_pool = stack.enter_context(tc.tile_pool(name="kinds", bufs=CHUNKS))
+        h_t_pool = stack.enter_context(tc.tile_pool(name="h_t", bufs=3))
+        kinds_pool = stack.enter_context(tc.tile_pool(name="kinds", bufs=4))
         h_rep_pool = stack.enter_context(tc.tile_pool(name="h_rep", bufs=REPLICAS))
         act_pool = stack.enter_context(tc.tile_pool(name="act", bufs=2))
         square_pool = stack.enter_context(tc.tile_pool(name="square", bufs=2))
@@ -155,20 +159,27 @@ def tile_kan1_pb_k_kernel(tc, h_mix, x, fc2_spline_w, fc2_base_w, fc2_base_b, ou
             centre_w.append(weights)
         h_rows_tiles = []
         for n in range(REPLICAS):
-            rows_tile = keep.tile([P, CHUNK_GROUPS, TENSOR_TOKENS], BF16, name="h_rows%d" % n)
+            rows_tile = keep.tile([P, ROUND_GROUPS, MAX_TENSOR_TOKENS], BF16, name="h_rows%d" % n)
             h_rows_tiles.append(rows_tile)
 
         def fill_ones(n):
-            nc.vector.memset(h_rows_tiles[n][3 * GROUP_HIDDEN : P], 1.0)
+            nc.gpsimd.memset(h_rows_tiles[n][3 * GROUP_HIDDEN : P], 1.0)
 
         fill_ones(0)
+        fill_ones(1)
 
         h_sb = []
 
         def load_hidden(quarter):
             h_quarter = keep.tile([P, TOKEN_TILES, K_PASS], BF16, name="h_quarter%d" % quarter)
-            cols = slice(quarter * K_PASS, (quarter + 1) * K_PASS)
-            nc.sync.dma_start(out=h_quarter[:], in_=h_rows[:, cols].rearrange("(t r) j -> r t j", r=P))
+            parts = 2 if quarter == 0 else 1
+            width = K_PASS // parts
+            for part in range(parts):
+                cols = slice(quarter * K_PASS + part * width, quarter * K_PASS + (part + 1) * width)
+                nc.sync.dma_start(
+                    out=h_quarter[:, :, part * width : (part + 1) * width],
+                    in_=h_rows[:, cols].rearrange("(t r) j -> r t j", r=P),
+                )
             h_sb.append(h_quarter)
 
 
@@ -194,46 +205,49 @@ def tile_kan1_pb_k_kernel(tc, h_mix, x, fc2_spline_w, fc2_base_w, fc2_base_b, ou
             nc.vector.tensor_copy(out=turned[:], in_=h_t_ps[:])
             h_t[chunk] = turned
 
-        def split_squares(chunk):
-            square = square_pool.tile([P, 2, TENSOR_TOKENS], F32)
-            nc.scalar.activation(out=square[:], in_=h_t[chunk][:, :, 0:TENSOR_TOKENS], func=ACT.Square)
-            kinds = kinds_pool.tile([P, 2, 2, TENSOR_TOKENS], BF16)
+        def hidden_units(r):
+            return h_t[r // CHUNK_ROUNDS][:, r % CHUNK_ROUNDS, :]
+
+        def split_squares(r):
+            tokens = tensor_tokens(r)
+            square = square_pool.tile([P, tokens], F32)
+            nc.scalar.activation(out=square[:], in_=hidden_units(r)[:, 0:tokens], func=ACT.Square)
+            kinds = kinds_pool.tile([P, 2, tokens], BF16)
             nc.gpsimd.tensor_scalar(
-                out=kinds[:, :, 0, :], in0=square[:], scalar1=1.0, scalar2=0.0, op0=ALU.mult, op1=ALU.add
+                out=kinds[:, 0, :], in0=square[:], scalar1=1.0, scalar2=0.0, op0=ALU.mult, op1=ALU.add
             )
-            nc.gpsimd.tensor_tensor(out=kinds[:, :, 1, :], in0=square[:], in1=kinds[:, :, 0, :], op=ALU.subtract)
-            h_kinds[chunk] = kinds
+            nc.gpsimd.tensor_tensor(out=kinds[:, 1, :], in0=square[:], in1=kinds[:, 0, :], op=ALU.subtract)
+            h_kinds[r] = kinds
 
-        def parked_rows(chunk, kind, words):
-            first_row = (2 * (chunk % PARK_SLOTS) + (kind > 0)) * CHUNK_HIDDEN
-            return out_rows[first_row : first_row + CHUNK_HIDDEN, words]
+        def parked_rows(r, kind, words):
+            first_row = (2 * (r % PARK_SLOTS) + (kind > 0)) * P
+            return out_rows[first_row : first_row + P, words]
 
-        def park_hidden(chunk):
+        def park_hidden(r):
+            nc.sync.dma_start(out=parked_rows(r, 0, slice(0, TOKENS // 2)), in_=hidden_units(r).bitcast(F32))
             nc.sync.dma_start(
-                out=parked_rows(chunk, 0, slice(0, TOKENS // 2)).rearrange("(a r) w -> r a w", r=P),
-                in_=h_t[chunk][:].bitcast(F32),
-            )
-            nc.sync.dma_start(
-                out=parked_rows(chunk, 1, slice(0, TENSOR_TOKENS)).rearrange("(a r) w -> r a w", r=P),
-                in_=h_kinds[chunk][:].rearrange("r a k n -> r a (k n)").bitcast(F32),
+                out=parked_rows(r, 1, slice(0, tensor_tokens(r))),
+                in_=h_kinds[r][:].rearrange("r k n -> r (k n)").bitcast(F32),
             )
 
-        def replicate_hidden(chunk):
-            half = TENSOR_TOKENS // 2
-            for kind, first_word in enumerate((0, 0, half)):
+        def replicate_hidden(r):
+            tokens = tensor_tokens(r)
+            for kind, first_word in enumerate((0, 0, tokens // 2)):
                 nc.sync.dma_start(
-                    out=h_rows_tiles[chunk % REPLICAS][kind * GROUP_HIDDEN : (kind + 1) * GROUP_HIDDEN].bitcast(F32),
-                    in_=parked_rows(chunk, kind, slice(first_word, first_word + half)).rearrange(
+                    out=h_rows_tiles[r % REPLICAS][
+                        kind * GROUP_HIDDEN : (kind + 1) * GROUP_HIDDEN, :, 0:tokens
+                    ].bitcast(F32),
+                    in_=parked_rows(r, kind, slice(first_word, first_word + tokens // 2)).rearrange(
                         "(a r) w -> r a w", r=GROUP_HIDDEN
                     ),
                 )
-            replicated = h_rep_pool.tile([P, CHUNK_GROUPS, ENGINE_TOKENS], BF16)
+            replicated = h_rep_pool.tile([P, ROUND_GROUPS, TOKENS - tokens], BF16)
             for copy in range(COPIES):
                 nc.sync.dma_start(
                     out=replicated[copy:P:COPIES, :, :].bitcast(F32),
-                    in_=parked_rows(chunk, 0, slice(half, TOKENS // 2)).rearrange("(a r) w -> r a w", r=GROUP_HIDDEN),
+                    in_=parked_rows(r, 0, slice(tokens // 2, TOKENS // 2)).rearrange("(a r) w -> r a w", r=GROUP_HIDDEN),
                 )
-            h_rep[chunk] = replicated
+            h_rep[r] = replicated
 
         w_raw = {}
         w_turned = {}
@@ -283,35 +297,33 @@ def tile_kan1_pb_k_kernel(tc, h_mix, x, fc2_spline_w, fc2_base_w, fc2_base_b, ou
             w_mx[i] = (w_codes, w_scales)
 
         def hidden_of_round(i):
-            r = order[i][1]
-            first = ROUND_GROUPS * (r % CHUNK_ROUNDS)
-            return h_rep[r // CHUNK_ROUNDS][:, first : first + ROUND_GROUPS, :].rearrange("q (a u) n -> q a n u", u=2)
+            return h_rep[order[i][1]][:].rearrange("q (a u) n -> q a n u", u=2)
 
         def exponents_on_tensor(i, a):
             r = order[i][1]
-            rows_tile = h_rows_tiles[(r // CHUNK_ROUNDS) % REPLICAS]
-            for block in range(TOKEN_BLOCKS):
+            for block in range(tensor_tokens(r) // BANK_TOKENS):
                 bank = turn_pool.tile([P, 2, 2, P], F32, tag="exponents")
                 tokens = slice(block * BANK_TOKENS, (block + 1) * BANK_TOKENS)
                 for e in range(2):
                     for u in range(2):
-                        group = ROUND_GROUPS * (r % CHUNK_ROUNDS) + 2 * a + u
                         nc.tensor.matmul(
-                            bank[:, u, e, 0:BANK_TOKENS],
+                            bank[:, u, e, :],
                             lhsT=centre_w[e][:].rearrange("r j i -> r (j i)"),
-                            rhs=rows_tile[:, group, tokens],
+                            rhs=h_rows_tiles[r % REPLICAS][:, 2 * a + u, tokens],
                             start=True,
                             stop=True,
                         )
                 exponents[i, a, block] = bank
 
         def square_on_scalar(i):
-            square = act_pool.tile([P, 2, ROUND_PASSES, ENGINE_TOKENS, 2], F32)
-            for e, first_token in ((1, 0), (0, DERIVED_TOKENS)):
-                if first_token < ENGINE_TOKENS:
+            r = order[i][1]
+            tokens = TOKENS - tensor_tokens(r)
+            square = act_pool.tile([P, 2, ROUND_PASSES, tokens, 2], F32)
+            for e, first_token in ((1, 0), (0, derived_tokens(r))):
+                if first_token < tokens:
                     nc.scalar.activation(
-                        out=square[:, e, :, first_token:ENGINE_TOKENS, :],
-                        in_=hidden_of_round(i)[:, :, first_token:ENGINE_TOKENS, :],
+                        out=square[:, e, :, first_token:tokens, :],
+                        in_=hidden_of_round(i)[:, :, first_token:tokens, :],
                         func=ACT.Square,
                         scale=SQUARE_SCALE,
                         bias=minus_centre[:, e : e + 1],
@@ -319,12 +331,13 @@ def tile_kan1_pb_k_kernel(tc, h_mix, x, fc2_spline_w, fc2_base_w, fc2_base_b, ou
             squares[i] = square
 
         def derive_on_vector(i):
+            tokens = slice(0, derived_tokens(order[i][1]))
             for a in range(ROUND_PASSES):
                 nc.vector.scalar_tensor_tensor(
-                    out=squares[i][:, 0, a, 0:DERIVED_TOKENS, :],
-                    in0=hidden_of_round(i)[:, a, 0:DERIVED_TOKENS, :],
+                    out=squares[i][:, 0, a, tokens, :],
+                    in0=hidden_of_round(i)[:, a, tokens, :],
                     scalar=step_const[:],
-                    in1=squares[i][:, 1, a, 0:DERIVED_TOKENS, :],
+                    in1=squares[i][:, 1, a, tokens, :],
                     op0=ALU.add,
                     op1=ALU.add,
                 )
@@ -333,17 +346,17 @@ def tile_kan1_pb_k_kernel(tc, h_mix, x, fc2_spline_w, fc2_base_w, fc2_base_b, ou
             if i not in basis:
                 basis_bf = act_pool.tile([P, ROUND_PASSES, TOKENS, PACK], BF16, align_bytes=64)
                 basis[i] = basis_bf
-            for block in range(TOKEN_BLOCKS):
+            for block in range(tensor_tokens(order[i][1]) // BANK_TOKENS):
                 nc.scalar.activation(
                     out=basis[i][:, a, block * BANK_TOKENS : (block + 1) * BANK_TOKENS, :],
-                    in_=exponents[i, a, block][:, :, :, 0:BANK_TOKENS].rearrange("q u e n -> q n (u e)"),
+                    in_=exponents[i, a, block][:].rearrange("q u e n -> q n (u e)"),
                     func=ACT.Exp,
                 )
 
         def exponentials_of_squares(i, passes):
             a = slice(passes.start, passes.stop)
             nc.scalar.activation(
-                out=basis[i][:, a, TENSOR_TOKENS:TOKENS, :].rearrange("q a n (u e) -> q a (n u) e", e=2),
+                out=basis[i][:, a, tensor_tokens(order[i][1]) : TOKENS, :].rearrange("q a n (u e) -> q a (n u) e", e=2),
                 in_=squares[i][:, :, a].rearrange("q e a n u -> q a (n u) e"),
                 func=ACT.Exp,
                 scale=-7.0,
@@ -407,61 +420,66 @@ def tile_kan1_pb_k_kernel(tc, h_mix, x, fc2_spline_w, fc2_base_w, fc2_base_b, ou
             passes = slice(b * ROUND_PASSES, (b + 1) * ROUND_PASSES)
             moving[order.index(("base", b))] = (silu_codes[:, passes, :], silu_scales[:, passes, :])
 
+        y_ps = [y_pool.tile([P, TOKENS], F32, name="y_ps%d" % m) for m in range(OUT_TILES)]
         load_hidden(0)
         load_weights(0)
         load_hidden(1)
         load_weights(1)
         load_hidden(2)
-        load_hidden(3)
-        y_ps = [y_pool.tile([P, TOKENS], F32, name="y_ps%d" % m) for m in range(OUT_TILES)]
-
-        for chunk in range(2):
-            turn_hidden(chunk)
-            keep_hidden(chunk)
-            split_squares(chunk)
-            park_hidden(chunk)
-            if chunk == 0:
-                load_weights(2)
-        fill_ones(1)
-        fill_ones(2)
+        turn_hidden(0)
+        keep_hidden(0)
+        split_squares(0)
+        park_hidden(0)
+        split_squares(1)
         make_silu(0)
+        park_hidden(1)
+        load_hidden(3)
         replicate_hidden(0)
-        replicate_hidden(1)
+        load_weights(2)
+        turn_hidden(1)
+        keep_hidden(1)
+        fill_ones(2)
+        fill_ones(3)
         for a in both:
             turn_weights(0, a)
             group_weights(0, a)
-        quantise_silu(0)
         make_silu(1)
-        quantise_weights(0)
+        quantise_silu(0)
         turn_weights(1, 0)
-        load_weights(3)
-        make_silu(2)
-        quantise_silu(1)
         group_weights(1, 0)
+        make_silu(2)
+        replicate_hidden(1)
+        quantise_weights(0)
         turn_weights(1, 1)
-        make_silu(3)
+        load_weights(3)
+        quantise_silu(1)
         group_weights(1, 1)
+        make_silu(3)
+        for r in range(2, 4):
+            split_squares(r)
+            park_hidden(r)
+        replicate_hidden(2)
         load_weights(4)
-        turn_weights(2, 0)
         quantise_weights(1)
         quantise_silu(2)
-        group_weights(2, 0)
-        turn_weights(2, 1)
-        quantise_silu(3)
-        load_weights(5)
         exponents_on_tensor(2, 0)
         square_on_scalar(2)
         exponentials_of_tensor(2, 0)
+        turn_weights(2, 0)
+        multiply(0, range(0, 2), both)
+        exponents_on_tensor(2, 1)
+        exponentials_of_tensor(2, 1)
+        quantise_silu(3)
+        derive_on_vector(2)
+        group_weights(2, 0)
+        turn_weights(2, 1)
+        multiply(0, range(2, OUT_TILES), both)
+        exponentials_of_squares(2, both)
+        load_weights(5)
         group_weights(2, 1)
         turn_hidden(2)
         keep_hidden(2)
-        exponents_on_tensor(2, 1)
-        exponentials_of_tensor(2, 1)
-        multiply(0, range(0, 2), both)
         turn_weights(3, 0)
-        derive_on_vector(2)
-        exponentials_of_squares(2, both)
-        multiply(0, range(2, OUT_TILES), both)
 
         for step in range(2, n_rounds - 1):
             if step > BASE_ROUNDS:
@@ -481,22 +499,23 @@ def tile_kan1_pb_k_kernel(tc, h_mix, x, fc2_spline_w, fc2_base_w, fc2_base_b, ou
             quantise_weights(step)
             group_weights(step + 1, 1)
             exponents_on_tensor(step + 1, 0)
-            ahead, odd = divmod(order[step + 1][1], CHUNK_ROUNDS)
-            if not odd and ahead + 2 < CHUNKS:
-                turn_hidden(ahead + 2)
+            r = order[step + 1][1]
+            chunk = r // CHUNK_ROUNDS + 2 if r % CHUNK_ROUNDS == 0 else CHUNKS
+            if chunk < CHUNKS:
+                turn_hidden(chunk)
             if step == n_rounds - 2:
                 bias_ps = turn_pool.tile([P, P], BF16, tag="turn")
                 nc.tensor.transpose(bias_ps[:], bias_rows[:], ident_bf[:])
                 bias_col = keep.tile([P, OUT_TILES], F32)
                 nc.vector.tensor_copy(out=bias_col[:], in_=bias_ps[:, 0:OUT_TILES])
             derive_on_vector(step + 1)
-            if not odd and ahead + 2 < CHUNKS:
-                keep_hidden(ahead + 2)
-            if odd and ahead + 2 < CHUNKS:
-                split_squares(ahead + 2)
-                park_hidden(ahead + 2)
-            if not odd and 1 <= ahead and ahead + 1 < CHUNKS:
-                replicate_hidden(ahead + 1)
+            if chunk < CHUNKS:
+                keep_hidden(chunk)
+            if r + 3 < SPLINE_ROUNDS:
+                split_squares(r + 3)
+                park_hidden(r + 3)
+            if r + 2 < SPLINE_ROUNDS:
+                replicate_hidden(r + 2)
             if is_round(step + 2):
                 turn_weights(step + 2, 0)
             if step > BASE_ROUNDS:

@@ -50,11 +50,11 @@ FLOPS = 2 * TOKENS * 512 * (HIDDEN * CENTRES + HIDDEN)
 
 
 def tensor_tokens(r):
-    return BANK_TOKENS if r % 4 == 3 else 2 * BANK_TOKENS
+    return BANK_TOKENS if r < 4 else 2 * BANK_TOKENS
 
 
 def derived_tokens(r):
-    return 320 if r % 4 == 3 else 256
+    return 288 if r < 4 else 224
 
 
 def quantise(nc, codes, scales, values):
@@ -479,6 +479,7 @@ def tile_kan1_pb_k_kernel(tc, h_mix, x, fc2_spline_w, fc2_base_w, fc2_base_b, ou
         group_weights(2, 1)
         turn_hidden(2)
         keep_hidden(2)
+        exponents_on_tensor(3, 0)
         turn_weights(3, 0)
 
         for step in range(2, n_rounds - 1):
@@ -498,7 +499,8 @@ def tile_kan1_pb_k_kernel(tc, h_mix, x, fc2_spline_w, fc2_base_w, fc2_base_b, ou
                 exponentials_of_tensor(step, 1)
             quantise_weights(step)
             group_weights(step + 1, 1)
-            exponents_on_tensor(step + 1, 0)
+            if step > BASE_ROUNDS:
+                exponents_on_tensor(step + 1, 0)
             r = order[step + 1][1]
             chunk = r // CHUNK_ROUNDS + 2 if r % CHUNK_ROUNDS == 0 else CHUNKS
             if chunk < CHUNKS:

@@ -25,6 +25,7 @@ HIDDEN = 2048
 CENTRES = 8
 OUT_TILES = 4
 CHANNELS = 256
+OUT_WORDS = TOKENS * 512
 
 ROUND_PASSES = 2
 ROUND_K = ROUND_PASSES * K_PASS
@@ -38,7 +39,8 @@ CHUNK_HIDDEN = 2 * P
 ROUND_GROUPS = 2 * ROUND_PASSES
 CHUNK_ROUNDS = CHUNK_HIDDEN // P
 CHUNKS = HIDDEN // CHUNK_HIDDEN
-PARK_SLOTS = 4
+PARK_SLOTS = 2
+SLOT_WORDS = OUT_WORDS // PARK_SLOTS
 REPLICAS = 4
 WEIGHTS_AHEAD = 3
 BANK_TOKENS = 128
@@ -54,7 +56,7 @@ def tensor_tokens(r):
 
 
 def derived_tokens(r):
-    return 288 if r < 4 else 224
+    return 256 if r < 4 else 192
 
 
 def quantise(nc, codes, scales, values):
@@ -65,8 +67,8 @@ def tile_kan1_pb_k_kernel(tc, h_mix, x, fc2_spline_w, fc2_base_w, fc2_base_b, ou
     nc = tc.nc
     h_rows = h_mix.flatten_outer_dims()
     x_rows = x.flatten_outer_dims().rearrange("(g r) c -> r g c", r=P)
-    out_rows = out.flatten_outer_dims()
-    out_tiles = out_rows.rearrange("(g r) c -> r g c", r=P)
+    out_words = out.rearrange("b p c -> (b p c)")
+    out_tiles = out.flatten_outer_dims().rearrange("(g r) c -> r g c", r=P)
 
     order = [("base", r) for r in range(BASE_ROUNDS)]
     for r in range(SPLINE_ROUNDS):
@@ -86,10 +88,11 @@ def tile_kan1_pb_k_kernel(tc, h_mix, x, fc2_spline_w, fc2_base_w, fc2_base_b, ou
         w_raw_pool = stack.enter_context(tc.tile_pool(name="w_raw", bufs=WEIGHTS_AHEAD))
         w_pool = stack.enter_context(tc.tile_pool(name="w", bufs=2))
         w_mx_pool = stack.enter_context(tc.tile_pool(name="w_mx", bufs=3))
-        h_t_pool = stack.enter_context(tc.tile_pool(name="h_t", bufs=3))
+        h_t_pool = stack.enter_context(tc.tile_pool(name="h_t", bufs=CHUNKS))
         kinds_pool = stack.enter_context(tc.tile_pool(name="kinds", bufs=4))
         h_rep_pool = stack.enter_context(tc.tile_pool(name="h_rep", bufs=REPLICAS))
         act_pool = stack.enter_context(tc.tile_pool(name="act", bufs=2))
+        basis_pool = stack.enter_context(tc.tile_pool(name="basis", bufs=3))
         square_pool = stack.enter_context(tc.tile_pool(name="square", bufs=2))
         act_mx_pool = stack.enter_context(tc.tile_pool(name="act_mx", bufs=2))
         res_pool = stack.enter_context(tc.tile_pool(name="res", bufs=OUT_TILES))
@@ -219,35 +222,48 @@ def tile_kan1_pb_k_kernel(tc, h_mix, x, fc2_spline_w, fc2_base_w, fc2_base_b, ou
             nc.gpsimd.tensor_tensor(out=kinds[:, 1, :], in0=square[:], in1=kinds[:, 0, :], op=ALU.subtract)
             h_kinds[r] = kinds
 
-        def parked_rows(r, kind, words):
-            first_row = (2 * (r % PARK_SLOTS) + (kind > 0)) * P
-            return out_rows[first_row : first_row + P, words]
+        def parked(r, first_word, words, width):
+            first = (r % PARK_SLOTS) * SLOT_WORDS + first_word
+            return out_words[first : first + words].rearrange("(r w) -> r w", w=width)
 
         def park_hidden(r):
-            nc.sync.dma_start(out=parked_rows(r, 0, slice(0, TOKENS // 2)), in_=hidden_units(r).bitcast(F32))
+            others = (TOKENS - tensor_tokens(r)) // 2
+            tensor = tensor_tokens(r) // 2
             nc.sync.dma_start(
-                out=parked_rows(r, 1, slice(0, tensor_tokens(r))),
+                out=parked(r, 0, P * COPIES * others, COPIES * others).rearrange("r (c w) -> r c w", c=COPIES),
+                in_=hidden_units(r)[:, tensor_tokens(r) : TOKENS]
+                .bitcast(F32)
+                .unsqueeze(1)
+                .to_broadcast([P, COPIES, others]),
+            )
+            kinds_at = P * COPIES * others
+            nc.sync.dma_start(
+                out=parked(r, kinds_at, P * tensor, tensor), in_=hidden_units(r)[:, 0 : tensor_tokens(r)].bitcast(F32)
+            )
+            nc.sync.dma_start(
+                out=parked(r, kinds_at + P * tensor, 2 * P * tensor, 2 * tensor),
                 in_=h_kinds[r][:].rearrange("r k n -> r (k n)").bitcast(F32),
             )
 
         def replicate_hidden(r):
-            tokens = tensor_tokens(r)
-            for kind, first_word in enumerate((0, 0, tokens // 2)):
+            others = (TOKENS - tensor_tokens(r)) // 2
+            tensor = tensor_tokens(r) // 2
+            replicated = h_rep_pool.tile([P, ROUND_GROUPS, TOKENS - tensor_tokens(r)], BF16)
+            nc.sync.dma_start(
+                out=replicated[:].bitcast(F32),
+                in_=parked(r, 0, P * COPIES * others, others).rearrange("(g q) w -> q g w", q=P),
+            )
+            h_rep[r] = replicated
+            kinds_at = P * COPIES * others
+            h_part = parked(r, kinds_at, P * tensor, tensor)
+            hi_lo = parked(r, kinds_at + P * tensor, 2 * P * tensor, 2 * tensor)
+            for kind, rows in enumerate((h_part, hi_lo[:, 0:tensor], hi_lo[:, tensor : 2 * tensor])):
                 nc.sync.dma_start(
                     out=h_rows_tiles[r % REPLICAS][
-                        kind * GROUP_HIDDEN : (kind + 1) * GROUP_HIDDEN, :, 0:tokens
+                        kind * GROUP_HIDDEN : (kind + 1) * GROUP_HIDDEN, :, 0 : 2 * tensor
                     ].bitcast(F32),
-                    in_=parked_rows(r, kind, slice(first_word, first_word + tokens // 2)).rearrange(
-                        "(a r) w -> r a w", r=GROUP_HIDDEN
-                    ),
+                    in_=rows.rearrange("(g r) w -> r g w", r=GROUP_HIDDEN),
                 )
-            replicated = h_rep_pool.tile([P, ROUND_GROUPS, TOKENS - tokens], BF16)
-            for copy in range(COPIES):
-                nc.sync.dma_start(
-                    out=replicated[copy:P:COPIES, :, :].bitcast(F32),
-                    in_=parked_rows(r, 0, slice(tokens // 2, TOKENS // 2)).rearrange("(a r) w -> r a w", r=GROUP_HIDDEN),
-                )
-            h_rep[r] = replicated
 
         w_raw = {}
         w_turned = {}
@@ -267,8 +283,8 @@ def tile_kan1_pb_k_kernel(tc, h_mix, x, fc2_spline_w, fc2_base_w, fc2_base_b, ou
             )
             w_raw[i] = raw
 
-        def turn_weights(i, a):
-            for half in range(2):
+        def turn_weights(i, a, halves=range(2)):
+            for half in halves:
                 w_t_ps = turn_pool.tile([P, 2, 2, P], F32, tag="turn")
                 for m in range(2):
                     for u in range(2):
@@ -344,7 +360,7 @@ def tile_kan1_pb_k_kernel(tc, h_mix, x, fc2_spline_w, fc2_base_w, fc2_base_b, ou
 
         def exponentials_of_tensor(i, a):
             if i not in basis:
-                basis_bf = act_pool.tile([P, ROUND_PASSES, TOKENS, PACK], BF16, align_bytes=64)
+                basis_bf = basis_pool.tile([P, ROUND_PASSES, TOKENS, PACK], BF16, align_bytes=64)
                 basis[i] = basis_bf
             for block in range(tensor_tokens(order[i][1]) // BANK_TOKENS):
                 nc.scalar.activation(
@@ -444,10 +460,12 @@ def tile_kan1_pb_k_kernel(tc, h_mix, x, fc2_spline_w, fc2_base_w, fc2_base_b, ou
             turn_weights(0, a)
             group_weights(0, a)
         make_silu(1)
+        split_squares(2)
         quantise_silu(0)
         turn_weights(1, 0)
         group_weights(1, 0)
         make_silu(2)
+        split_squares(3)
         replicate_hidden(1)
         quantise_weights(0)
         turn_weights(1, 1)
@@ -456,12 +474,11 @@ def tile_kan1_pb_k_kernel(tc, h_mix, x, fc2_spline_w, fc2_base_w, fc2_base_b, ou
         group_weights(1, 1)
         make_silu(3)
         for r in range(2, 4):
-            split_squares(r)
             park_hidden(r)
         replicate_hidden(2)
         load_weights(4)
-        quantise_weights(1)
         quantise_silu(2)
+        quantise_weights(1)
         exponents_on_tensor(2, 0)
         square_on_scalar(2)
         exponentials_of_tensor(2, 0)
@@ -482,44 +499,42 @@ def tile_kan1_pb_k_kernel(tc, h_mix, x, fc2_spline_w, fc2_base_w, fc2_base_b, ou
         exponents_on_tensor(3, 0)
         turn_weights(3, 0)
 
+        turned = CHUNKS
         for step in range(2, n_rounds - 1):
             if step > BASE_ROUNDS:
                 exponentials_of_tensor(step, 0)
                 exponents_on_tensor(step, 1)
             if is_spline(step - 1):
                 quantise_basis(step - 1, both)
+            if turned < CHUNKS:
+                keep_hidden(turned)
+                turn_weights(step + 1, 0, range(1, 2))
             multiply(step - 1, range(0, 1), both)
             group_weights(step + 1, 0)
             turn_weights(step + 1, 1)
             if is_round(step + 1 + WEIGHTS_AHEAD):
                 load_weights(step + 1 + WEIGHTS_AHEAD)
-            multiply(step - 1, range(1, OUT_TILES), both)
             square_on_scalar(step + 1)
             if step > BASE_ROUNDS:
                 exponentials_of_tensor(step, 1)
-            quantise_weights(step)
-            group_weights(step + 1, 1)
             if step > BASE_ROUNDS:
                 exponents_on_tensor(step + 1, 0)
+            multiply(step - 1, range(1, OUT_TILES), both)
+            quantise_weights(step)
+            group_weights(step + 1, 1)
             r = order[step + 1][1]
             chunk = r // CHUNK_ROUNDS + 2 if r % CHUNK_ROUNDS == 0 else CHUNKS
+            turned = chunk
             if chunk < CHUNKS:
                 turn_hidden(chunk)
-            if step == n_rounds - 2:
-                bias_ps = turn_pool.tile([P, P], BF16, tag="turn")
-                nc.tensor.transpose(bias_ps[:], bias_rows[:], ident_bf[:])
-                bias_col = keep.tile([P, OUT_TILES], F32)
-                nc.vector.tensor_copy(out=bias_col[:], in_=bias_ps[:, 0:OUT_TILES])
             derive_on_vector(step + 1)
-            if chunk < CHUNKS:
-                keep_hidden(chunk)
             if r + 3 < SPLINE_ROUNDS:
                 split_squares(r + 3)
                 park_hidden(r + 3)
             if r + 2 < SPLINE_ROUNDS:
                 replicate_hidden(r + 2)
             if is_round(step + 2):
-                turn_weights(step + 2, 0)
+                turn_weights(step + 2, 0, range(1) if chunk < CHUNKS else range(2))
             if step > BASE_ROUNDS:
                 exponentials_of_squares(step, both)
             if step == 4:
@@ -529,6 +544,10 @@ def tile_kan1_pb_k_kernel(tc, h_mix, x, fc2_spline_w, fc2_base_w, fc2_base_b, ou
                 x_sb = keep.tile([P, 2 * OUT_TILES, CHANNELS], BF16)
                 nc.sync.dma_start(out=x_sb[:], in_=x_rows)
 
+        bias_ps = turn_pool.tile([P, P], BF16, tag="turn")
+        nc.tensor.transpose(bias_ps[:], bias_rows[:], ident_bf[:])
+        bias_col = keep.tile([P, OUT_TILES], F32)
+        nc.vector.tensor_copy(out=bias_col[:], in_=bias_ps[:, 0:OUT_TILES])
         final = n_rounds - 1
         quantise_basis(final - 1, both)
         quantise_weights(final)

@@ -55,8 +55,12 @@ def tensor_tokens(r):
     return BANK_TOKENS if r < 4 else 2 * BANK_TOKENS
 
 
+def parked_copies(r):
+    return 1 if r < 4 else COPIES
+
+
 def derived_tokens(r):
-    return 256 if r < 4 else 192
+    return 224 if r < 4 else 160
 
 
 def quantise(nc, codes, scales, values):
@@ -214,7 +218,9 @@ def tile_kan1_pb_k_kernel(tc, h_mix, x, fc2_spline_w, fc2_base_w, fc2_base_b, ou
         def split_squares(r):
             tokens = tensor_tokens(r)
             square = square_pool.tile([P, tokens], F32)
-            nc.scalar.activation(out=square[:], in_=hidden_units(r)[:, 0:tokens], func=ACT.Square)
+            nc.gpsimd.tensor_tensor(
+                out=square[:], in0=hidden_units(r)[:, 0:tokens], in1=hidden_units(r)[:, 0:tokens], op=ALU.mult
+            )
             kinds = kinds_pool.tile([P, 2, tokens], BF16)
             nc.gpsimd.tensor_scalar(
                 out=kinds[:, 0, :], in0=square[:], scalar1=1.0, scalar2=0.0, op0=ALU.mult, op1=ALU.add
@@ -229,12 +235,13 @@ def tile_kan1_pb_k_kernel(tc, h_mix, x, fc2_spline_w, fc2_base_w, fc2_base_b, ou
         def park_hidden(r):
             others = (TOKENS - tensor_tokens(r)) // 2
             tensor = tensor_tokens(r) // 2
+            copies = parked_copies(r)
             nc.sync.dma_start(
-                out=parked(r, 0, P * COPIES * others, COPIES * others).rearrange("r (c w) -> r c w", c=COPIES),
+                out=parked(r, 0, P * copies * others, copies * others).rearrange("r (c w) -> r c w", c=copies),
                 in_=hidden_units(r)[:, tensor_tokens(r) : TOKENS]
                 .bitcast(F32)
                 .unsqueeze(1)
-                .to_broadcast([P, COPIES, others]),
+                .to_broadcast([P, copies, others]),
             )
             kinds_at = P * COPIES * others
             nc.sync.dma_start(
@@ -249,10 +256,12 @@ def tile_kan1_pb_k_kernel(tc, h_mix, x, fc2_spline_w, fc2_base_w, fc2_base_b, ou
             others = (TOKENS - tensor_tokens(r)) // 2
             tensor = tensor_tokens(r) // 2
             replicated = h_rep_pool.tile([P, ROUND_GROUPS, TOKENS - tensor_tokens(r)], BF16)
-            nc.sync.dma_start(
-                out=replicated[:].bitcast(F32),
-                in_=parked(r, 0, P * COPIES * others, others).rearrange("(g q) w -> q g w", q=P),
-            )
+            copies = parked_copies(r)
+            for copy in range(COPIES // copies):
+                nc.sync.dma_start(
+                    out=replicated[copy : P : COPIES // copies].bitcast(F32),
+                    in_=parked(r, 0, P * copies * others, others).rearrange("(g q) w -> q g w", q=GROUP_HIDDEN * copies),
+                )
             h_rep[r] = replicated
             kinds_at = P * COPIES * others
             h_part = parked(r, kinds_at, P * tensor, tensor)
@@ -528,16 +537,16 @@ def tile_kan1_pb_k_kernel(tc, h_mix, x, fc2_spline_w, fc2_base_w, fc2_base_b, ou
             if chunk < CHUNKS:
                 turn_hidden(chunk)
             derive_on_vector(step + 1)
+            if r + 2 < SPLINE_ROUNDS:
+                replicate_hidden(r + 2)
             if r + 3 < SPLINE_ROUNDS:
                 split_squares(r + 3)
                 park_hidden(r + 3)
-            if r + 2 < SPLINE_ROUNDS:
-                replicate_hidden(r + 2)
             if is_round(step + 2):
                 turn_weights(step + 2, 0, range(1) if chunk < CHUNKS else range(2))
             if step > BASE_ROUNDS:
                 exponentials_of_squares(step, both)
-            if step == 4:
+            if step == 10:
                 bias_rows = keep.tile([P, P], BF16)
                 nc.gpsimd.memset(bias_rows[:], 0.0)
                 nc.sync.dma_start(out=bias_rows[0:OUT_TILES, :], in_=fc2_base_b.rearrange("(m r) -> m r", r=P))

from contextlib import ExitStack

import math

import concourse.mybir as mybir
from concourse.masks import make_identity

F32 = mybir.dt.float32
BF16 = mybir.dt.bfloat16
I32 = mybir.dt.int32
U32 = mybir.dt.uint32
U8 = mybir.dt.uint8
FP8X4 = mybir.dt.float8_e4m3fn_x4
ACT = mybir.ActivationFunctionType
ALU = mybir.AluOpType

P = 128
PACK = 4
K_PASS = P * PACK
WORDS = K_PASS // 2

TOKENS = 512
TOKEN_TILES = TOKENS // P
HIDDEN = 2048
CENTRES = 8
OUT_TILES = 4
CHANNELS = 256
OUT_WORDS = TOKENS * 512

ROUND_PASSES = 2
ROUND_K = ROUND_PASSES * K_PASS
BASE_PASSES = HIDDEN // K_PASS
BASE_ROUNDS = BASE_PASSES // ROUND_PASSES
SPLINE_ROUNDS = HIDDEN * CENTRES // ROUND_K

COPIES = 4
GROUP_HIDDEN = P // COPIES
CHUNK_HIDDEN = 2 * P
ROUND_GROUPS = 2 * ROUND_PASSES
CHUNK_ROUNDS = CHUNK_HIDDEN // P
CHUNKS = HIDDEN // CHUNK_HIDDEN
PARK_SLOTS = 2
SLOT_WORDS = OUT_WORDS // PARK_SLOTS
REPLICAS = 4
WEIGHTS_AHEAD = 3
BANK_TOKENS = 128
MAX_TENSOR_TOKENS = 2 * BANK_TOKENS

SQUARE_SCALE = 3.5 / math.sqrt(7.0)

FLOPS = 2 * TOKENS * 512 * (HIDDEN * CENTRES + HIDDEN)


def tensor_tokens(r):
    return BANK_TOKENS if r < 4 else 2 * BANK_TOKENS


def parked_copies(r):
    return 1 if r < 4 else COPIES


def derived_tokens(r):
    return 224 if r < 4 else 160


def quantise(nc, codes, scales, values):
    nc.vector.quantize_mx(out=codes.bitcast(FP8X4), scales=scales, in_=values)


def tile_kan1_pb_k_kernel(tc, h_mix, x, fc2_spline_w, fc2_base_w, fc2_base_b, out):
    nc = tc.nc
    h_rows = h_mix.flatten_outer_dims()
    x_rows = x.flatten_outer_dims().rearrange("(g r) c -> r g c", r=P)
    out_words = out.rearrange("b p c -> (b p c)")
    out_tiles = out.flatten_outer_dims().rearrange("(g r) c -> r g c", r=P)

    order = [("base", r) for r in range(BASE_ROUNDS)]
    for r in range(SPLINE_ROUNDS):
        order.append(("spline", r))
    n_rounds = len(order)

    def is_round(i):
        return 0 <= i < n_rounds

    def is_spline(i):
        return is_round(i) and order[i][0] == "spline"

    both = range(ROUND_PASSES)

    with ExitStack() as stack:
        keep = stack.enter_context(tc.tile_pool(name="keep", bufs=1))
        w_raw_pool = stack.enter_context(tc.tile_pool(name="w_raw", bufs=WEIGHTS_AHEAD))
        w_pool = stack.enter_context(tc.tile_pool(name="w", bufs=2))
        w_mx_pool = stack.enter_context(tc.tile_pool(name="w_mx", bufs=3))
        h_t_pool = stack.enter_context(tc.tile_pool(name="h_t", bufs=CHUNKS))
        kinds_pool = stack.enter_context(tc.tile_pool(name="kinds", bufs=4))
        h_rep_pool = stack.enter_context(tc.tile_pool(name="h_rep", bufs=REPLICAS))
        act_pool = stack.enter_context(tc.tile_pool(name="act", bufs=2))
        basis_pool = stack.enter_context(tc.tile_pool(name="basis", bufs=3))
        square_pool = stack.enter_context(tc.tile_pool(name="square", bufs=2))
        act_mx_pool = stack.enter_context(tc.tile_pool(name="act_mx", bufs=2))
        res_pool = stack.enter_context(tc.tile_pool(name="res", bufs=OUT_TILES))
        y_pool = stack.enter_context(tc.psum_pool(name="y", bufs=1))
        turn_pool = stack.enter_context(tc.psum_pool(name="turn", bufs=2))
        stack.enter_context(tc.manual_schedule())

        part_idx = keep.tile([P, 1], I32)
        nc.gpsimd.iota(part_idx[:], pattern=[[0, 1]], base=0, channel_multiplier=1)
        part_mod = keep.tile([P, 1], I32)
        nc.vector.tensor_single_scalar(out=part_mod[:], in_=part_idx[:], scalar=COPIES - 1, op=ALU.bitwise_and)
        part_mod_f = keep.tile([P, 1], F32)
        nc.vector.tensor_copy(out=part_mod_f[:], in_=part_mod[:])
        minus_centre = keep.tile([P, 2], F32)
        for e in range(2):
            nc.vector.tensor_scalar(
                out=minus_centre[:, e : e + 1],
                in0=part_mod_f[:],
                scalar1=-2.0 / math.sqrt(7.0),
                scalar2=(3.5 - e) / math.sqrt(7.0),
                op0=ALU.mult,
                op1=ALU.add,
            )
        step_const = keep.tile([P, 1], F32)
        nc.vector.tensor_scalar(
            out=step_const[:], in0=part_mod_f[:], scalar1=-4.0 / 7.0, scalar2=6.0 / 7.0, op0=ALU.mult, op1=ALU.add
        )
        ident_bf = keep.tile([P, P], BF16)
        make_identity(nc, ident_bf[:])
        ident_f32 = keep.tile([P, P], F32)
        make_identity(nc, ident_f32[:])

        twice_place = keep.tile([P, GROUP_HIDDEN, COPIES], F32)
        nc.gpsimd.iota(
            twice_place[:],
            pattern=[[0, GROUP_HIDDEN], [2, COPIES]],
            base=0,
            channel_multiplier=0,
            allow_small_or_imprecise_dtypes=True,
        )
        centre_w = []
        for e in range(2):
            weights = keep.tile([P, GROUP_HIDDEN, COPIES], BF16, name="centre_w%d" % e)
            seven_c = keep.tile([P, GROUP_HIDDEN, COPIES], F32, name="seven_c%d" % e)
            nc.vector.tensor_scalar(
                out=seven_c[:], in0=twice_place[:], scalar1=e - 3.5, scalar2=7.0, op0=ALU.add, op1=ALU.mult
            )
            for kind in range(3):
                rows = slice(kind * GROUP_HIDDEN, (kind + 1) * GROUP_HIDDEN)
                unit = ident_bf[rows, rows].unsqueeze(2).to_broadcast([GROUP_HIDDEN, GROUP_HIDDEN, COPIES])
                if kind == 0:
                    nc.vector.tensor_tensor(out=weights[rows], in0=seven_c[rows], in1=unit, op=ALU.mult)
                else:
                    nc.vector.tensor_scalar(
                        out=weights[rows], in0=unit, scalar1=-12.25, scalar2=0.0, op0=ALU.mult, op1=ALU.add
                    )
            nc.vector.memset(weights[3 * GROUP_HIDDEN : P], 0.0)
            ones_row = slice(3 * GROUP_HIDDEN, 3 * GROUP_HIDDEN + 1)
            nc.vector.scalar_tensor_tensor(
                out=weights[ones_row],
                in0=seven_c[ones_row],
                scalar=-1.0 / 49.0,
                in1=seven_c[ones_row],
                op0=ALU.mult,
                op1=ALU.mult,
            )
            centre_w.append(weights)
        h_rows_tiles = []
        for n in range(REPLICAS):
            rows_tile = keep.tile([P, ROUND_GROUPS, MAX_TENSOR_TOKENS], BF16, name="h_rows%d" % n)
            h_rows_tiles.append(rows_tile)

        def fill_ones(n):
            nc.gpsimd.memset(h_rows_tiles[n][3 * GROUP_HIDDEN : P], 1.0)

        fill_ones(0)
        fill_ones(1)

        h_sb = []

        def load_hidden(quarter):
            h_quarter = keep.tile([P, TOKEN_TILES, K_PASS], BF16, name="h_quarter%d" % quarter)
            parts = 2 if quarter == 0 else 1
            width = K_PASS // parts
            for part in range(parts):
                cols = slice(quarter * K_PASS + part * width, quarter * K_PASS + (part + 1) * width)
                nc.sync.dma_start(
                    out=h_quarter[:, :, part * width : (part + 1) * width],
                    in_=h_rows[:, cols].rearrange("(t r) j -> r t j", r=P),
                )
            h_sb.append(h_quarter)


        h_turned = {}
        h_t = {}
        h_kinds = {}
        h_rep = {}

        def turn_hidden(chunk):
            h_t_ps = turn_pool.tile([P, 2, TOKENS], BF16, tag="turn")
            quarter, first_hidden = divmod(chunk * CHUNK_HIDDEN, K_PASS)
            for half in range(2):
                first = first_hidden + half * P
                for t in range(TOKEN_TILES):
                    nc.tensor.transpose(
                        h_t_ps[:, half, t * P : (t + 1) * P], h_sb[quarter][:, t, first : first + P], ident_bf[:]
                    )
            h_turned[chunk] = h_t_ps

        def keep_hidden(chunk):
            h_t_ps = h_turned[chunk]
            turned = h_t_pool.tile([P, 2, TOKENS], BF16)
            nc.vector.tensor_copy(out=turned[:], in_=h_t_ps[:])
            h_t[chunk] = turned

        def hidden_units(r):
            return h_t[r // CHUNK_ROUNDS][:, r % CHUNK_ROUNDS, :]

        def split_squares(r):
            tokens = tensor_tokens(r)
            square = square_pool.tile([P, tokens], F32)
            nc.gpsimd.tensor_tensor(
                out=square[:], in0=hidden_units(r)[:, 0:tokens], in1=hidden_units(r)[:, 0:tokens], op=ALU.mult
            )
            kinds = kinds_pool.tile([P, 2, tokens], BF16)
            nc.gpsimd.tensor_scalar(
                out=kinds[:, 0, :], in0=square[:], scalar1=1.0, scalar2=0.0, op0=ALU.mult, op1=ALU.add
            )
            nc.gpsimd.tensor_tensor(out=kinds[:, 1, :], in0=square[:], in1=kinds[:, 0, :], op=ALU.subtract)
            h_kinds[r] = kinds

        def parked(r, first_word, words, width):
            first = (r % PARK_SLOTS) * SLOT_WORDS + first_word
            return out_words[first : first + words].rearrange("(r w) -> r w", w=width)

        def park_hidden(r):
            others = (TOKENS - tensor_tokens(r)) // 2
            tensor = tensor_tokens(r) // 2
            copies = parked_copies(r)
            nc.sync.dma_start(
                out=parked(r, 0, P * copies * others, copies * others).rearrange("r (c w) -> r c w", c=copies),
                in_=hidden_units(r)[:, tensor_tokens(r) : TOKENS]
                .bitcast(F32)
                .unsqueeze(1)
                .to_broadcast([P, copies, others]),
            )
            kinds_at = P * COPIES * others
            nc.sync.dma_start(
                out=parked(r, kinds_at, P * tensor, tensor), in_=hidden_units(r)[:, 0 : tensor_tokens(r)].bitcast(F32)
            )
            nc.sync.dma_start(
                out=parked(r, kinds_at + P * tensor, 2 * P * tensor, 2 * tensor),
                in_=h_kinds[r][:].rearrange("r k n -> r (k n)").bitcast(F32),
            )

        def replicate_hidden(r):
            others = (TOKENS - tensor_tokens(r)) // 2
            tensor = tensor_tokens(r) // 2
            replicated = h_rep_pool.tile([P, ROUND_GROUPS, TOKENS - tensor_tokens(r)], BF16)
            copies = parked_copies(r)
            for copy in range(COPIES // copies):
                nc.sync.dma_start(
                    out=replicated[copy : P : COPIES // copies].bitcast(F32),
                    in_=parked(r, 0, P * copies * others, others).rearrange("(g q) w -> q g w", q=GROUP_HIDDEN * copies),
                )
            h_rep[r] = replicated
            kinds_at = P * COPIES * others
            h_part = parked(r, kinds_at, P * tensor, tensor)
            hi_lo = parked(r, kinds_at + P * tensor, 2 * P * tensor, 2 * tensor)
            for kind, rows in enumerate((h_part, hi_lo[:, 0:tensor], hi_lo[:, tensor : 2 * tensor])):
                nc.sync.dma_start(
                    out=h_rows_tiles[r % REPLICAS][
                        kind * GROUP_HIDDEN : (kind + 1) * GROUP_HIDDEN, :, 0 : 2 * tensor
                    ].bitcast(F32),
                    in_=rows.rearrange("(g r) w -> r g w", r=GROUP_HIDDEN),
                )

        w_raw = {}
        w_turned = {}
        w_grouped = {}
        w_mx = {}
        exponents = {}
        squares = {}
        basis = {}
        moving = {}

        def load_weights(i):
            kind, r = order[i]
            w_dram = fc2_base_w if kind == "base" else fc2_spline_w
            raw = w_raw_pool.tile([P, OUT_TILES, ROUND_K], BF16)
            nc.sync.dma_start(
                out=raw[:], in_=w_dram[:, r * ROUND_K : (r + 1) * ROUND_K].rearrange("(m r) k -> r m k", r=P)
            )
            w_raw[i] = raw

        def turn_weights(i, a, halves=range(2)):
            for half in halves:
                w_t_ps = turn_pool.tile([P, 2, 2, P], F32, tag="turn")
                for m in range(2):
                    for u in range(2):
                        first = a * WORDS + u * P
                        nc.tensor.transpose(
                            w_t_ps[:, m, u, :],
                            w_raw[i][:, 2 * half + m, :].bitcast(F32)[:, first : first + P],
                            ident_f32[:],
                        )
                w_turned[i, a, half] = w_t_ps

        def group_weights(i, a):
            if i not in w_grouped:
                w_bf = w_pool.tile([P, ROUND_PASSES * OUT_TILES * P * PACK], BF16, align_bytes=64)
                w_grouped[i] = w_bf
            w_words = w_grouped[i][:].bitcast(F32).rearrange("q (b m r u) -> q b m r u", m=2, r=P, u=2)
            for half in range(2):
                nc.vector.tensor_copy(
                    out=w_words[:, 2 * a + half], in_=w_turned[i, a, half][:].rearrange("q m u r -> q m r u")
                )

        def quantise_weights(i):
            w_codes = w_mx_pool.tile([P, ROUND_PASSES * OUT_TILES * P], U32, align_bytes=64)
            w_scales = w_mx_pool.tile([P, ROUND_PASSES * OUT_TILES * P], U8, align_bytes=64)
            quantise(nc, w_codes[:], w_scales[:], w_grouped[i][:])
            w_mx[i] = (w_codes, w_scales)

        def hidden_of_round(i):
            return h_rep[order[i][1]][:].rearrange("q (a u) n -> q a n u", u=2)

        def exponents_on_tensor(i, a):
            r = order[i][1]
            for block in range(tensor_tokens(r) // BANK_TOKENS):
                bank = turn_pool.tile([P, 2, 2, P], F32, tag="exponents")
                tokens = slice(block * BANK_TOKENS, (block + 1) * BANK_TOKENS)
                for e in range(2):
                    for u in range(2):
                        nc.tensor.matmul(
                            bank[:, u, e, :],
                            lhsT=centre_w[e][:].rearrange("r j i -> r (j i)"),
                            rhs=h_rows_tiles[r % REPLICAS][:, 2 * a + u, tokens],
                            start=True,
                            stop=True,
                        )
                exponents[i, a, block] = bank

        def square_on_scalar(i):
            r = order[i][1]
            tokens = TOKENS - tensor_tokens(r)
            square = act_pool.tile([P, 2, ROUND_PASSES, tokens, 2], F32)
            for e, first_token in ((1, 0), (0, derived_tokens(r))):
                if first_token < tokens:
                    nc.scalar.activation(
                        out=square[:, e, :, first_token:tokens, :],
                        in_=hidden_of_round(i)[:, :, first_token:tokens, :],
                        func=ACT.Square,
                        scale=SQUARE_SCALE,
                        bias=minus_centre[:, e : e + 1],
                    )
            squares[i] = square

        def derive_on_vector(i):
            tokens = slice(0, derived_tokens(order[i][1]))
            for a in range(ROUND_PASSES):
                nc.vector.scalar_tensor_tensor(
                    out=squares[i][:, 0, a, tokens, :],
                    in0=hidden_of_round(i)[:, a, tokens, :],
                    scalar=step_const[:],
                    in1=squares[i][:, 1, a, tokens, :],
                    op0=ALU.add,
                    op1=ALU.add,
                )

        def exponentials_of_tensor(i, a):
            if i not in basis:
                basis_bf = basis_pool.tile([P, ROUND_PASSES, TOKENS, PACK], BF16, align_bytes=64)
                basis[i] = basis_bf
            for block in range(tensor_tokens(order[i][1]) // BANK_TOKENS):
                nc.scalar.activation(
                    out=basis[i][:, a, block * BANK_TOKENS : (block + 1) * BANK_TOKENS, :],
                    in_=exponents[i, a, block][:].rearrange("q u e n -> q n (u e)"),
                    func=ACT.Exp,
                )

        def exponentials_of_squares(i, passes):
            a = slice(passes.start, passes.stop)
            nc.scalar.activation(
                out=basis[i][:, a, tensor_tokens(order[i][1]) : TOKENS, :].rearrange("q a n (u e) -> q a (n u) e", e=2),
                in_=squares[i][:, :, a].rearrange("q e a n u -> q a (n u) e"),
                func=ACT.Exp,
                scale=-7.0,
            )

        def quantise_basis(i, passes):
            if i not in moving:
                codes = act_mx_pool.tile([P, ROUND_PASSES, TOKENS], U32, align_bytes=64)
                scales = act_mx_pool.tile([P, ROUND_PASSES, TOKENS], U8, align_bytes=64)
                moving[i] = (codes[:], scales[:])
            a = slice(passes.start, passes.stop)
            quantise(
                nc,
                moving[i][0][:, a].rearrange("q a n -> q (a n)"),
                moving[i][1][:, a].rearrange("q a n -> q (a n)"),
                basis[i][:, a].rearrange("q a n t -> q (a n t)"),
            )

        def multiply(i, tiles, passes):
            w_codes, w_scales = w_mx[i]
            codes, scales = moving[i]
            for m in tiles:
                for a in passes:
                    cols = slice((a * OUT_TILES + m) * P, (a * OUT_TILES + m + 1) * P)
                    nc.tensor.matmul_mx(
                        out=y_ps[m][:],
                        lhsT=w_codes[:, cols].bitcast(FP8X4),
                        lhsT_scale=w_scales[:, cols],
                        rhs=codes[:, a, :].bitcast(FP8X4),
                        rhs_scale=scales[:, a, :],
                        start=(i == 0 and a == 0),
                        stop=(i == n_rounds - 1 and a == ROUND_PASSES - 1),
                    )

        silu_codes = keep.tile([P, BASE_PASSES, TOKENS], U32, align_bytes=64)
        silu_scales = keep.tile([P, BASE_PASSES, TOKENS], U8, align_bytes=64)
        silu = {}

        def make_silu(g):
            silu_bf = act_pool.tile([P, TOKENS, PACK], BF16, align_bytes=64)
            for half in range(2):
                h_w_ps = turn_pool.tile([P, 2, 2 * P], F32, tag="exponents")
                for u in range(2):
                    for t in range(2):
                        nc.tensor.transpose(
                            h_w_ps[:, u, t * P : (t + 1) * P],
                            h_sb[g][:, 2 * half + t, :].bitcast(F32)[:, u * P : (u + 1) * P],
                            ident_f32[:],
                        )
                nc.scalar.activation(
                    out=silu_bf[:, half * 2 * P : (half + 1) * 2 * P, :].rearrange("q n (u e) -> q n u e", u=2),
                    in_=h_w_ps[:].bitcast(BF16).rearrange("q u (n e) -> q n u e", e=2),
                    func=ACT.Silu,
                )
            silu[g] = silu_bf

        def quantise_silu(g):
            quantise(nc, silu_codes[:, g, :], silu_scales[:, g, :], silu[g][:].rearrange("q n t -> q (n t)"))

        for b in range(BASE_ROUNDS):
            passes = slice(b * ROUND_PASSES, (b + 1) * ROUND_PASSES)
            moving[order.index(("base", b))] = (silu_codes[:, passes, :], silu_scales[:, passes, :])

        y_ps = [y_pool.tile([P, TOKENS], F32, name="y_ps%d" % m) for m in range(OUT_TILES)]
        load_hidden(0)
        load_weights(0)
        load_hidden(1)
        load_weights(1)
        load_hidden(2)
        turn_hidden(0)
        keep_hidden(0)
        split_squares(0)
        park_hidden(0)
        split_squares(1)
        make_silu(0)
        park_hidden(1)
        load_hidden(3)
        replicate_hidden(0)
        load_weights(2)
        turn_hidden(1)
        keep_hidden(1)
        fill_ones(2)
        fill_ones(3)
        for a in both:
            turn_weights(0, a)
            group_weights(0, a)
        make_silu(1)
        split_squares(2)
        quantise_silu(0)
        turn_weights(1, 0)
        group_weights(1, 0)
        make_silu(2)
        split_squares(3)
        replicate_hidden(1)
        quantise_weights(0)
        turn_weights(1, 1)
        load_weights(3)
        quantise_silu(1)
        group_weights(1, 1)
        make_silu(3)
        for r in range(2, 4):
            park_hidden(r)
        replicate_hidden(2)
        load_weights(4)
        quantise_silu(2)
        quantise_weights(1)
        exponents_on_tensor(2, 0)
        square_on_scalar(2)
        exponentials_of_tensor(2, 0)
        turn_weights(2, 0)
        multiply(0, range(0, 2), both)
        exponents_on_tensor(2, 1)
        exponentials_of_tensor(2, 1)
        quantise_silu(3)
        derive_on_vector(2)
        group_weights(2, 0)
        turn_weights(2, 1)
        multiply(0, range(2, OUT_TILES), both)
        exponentials_of_squares(2, both)
        load_weights(5)
        group_weights(2, 1)
        turn_hidden(2)
        keep_hidden(2)
        exponents_on_tensor(3, 0)
        turn_weights(3, 0)

        turned = CHUNKS
        for step in range(2, n_rounds - 1):
            if step > BASE_ROUNDS:
                exponentials_of_tensor(step, 0)
                exponents_on_tensor(step, 1)
            if is_spline(step - 1):
                quantise_basis(step - 1, both)
            if turned < CHUNKS:
                keep_hidden(turned)
                turn_weights(step + 1, 0, range(1, 2))
            multiply(step - 1, range(0, 1), both)
            group_weights(step + 1, 0)
            turn_weights(step + 1, 1)
            if is_round(step + 1 + WEIGHTS_AHEAD):
                load_weights(step + 1 + WEIGHTS_AHEAD)
            square_on_scalar(step + 1)
            if step > BASE_ROUNDS:
                exponentials_of_tensor(step, 1)
            if step > BASE_ROUNDS:
                exponents_on_tensor(step + 1, 0)
            multiply(step - 1, range(1, OUT_TILES), both)
            quantise_weights(step)
            group_weights(step + 1, 1)
            r = order[step + 1][1]
            chunk = r // CHUNK_ROUNDS + 2 if r % CHUNK_ROUNDS == 0 else CHUNKS
            turned = chunk
            if chunk < CHUNKS:
                turn_hidden(chunk)
            derive_on_vector(step + 1)
            if r + 2 < SPLINE_ROUNDS:
                replicate_hidden(r + 2)
            if r + 3 < SPLINE_ROUNDS:
                split_squares(r + 3)
                park_hidden(r + 3)
            if is_round(step + 2):
                turn_weights(step + 2, 0, range(1) if chunk < CHUNKS else range(2))
            if step > BASE_ROUNDS:
                exponentials_of_squares(step, both)
            if step == 10:
                bias_rows = keep.tile([P, P], BF16)
                nc.gpsimd.memset(bias_rows[:], 0.0)
                nc.sync.dma_start(out=bias_rows[0:OUT_TILES, :], in_=fc2_base_b.rearrange("(m r) -> m r", r=P))
                x_sb = keep.tile([P, 2 * OUT_TILES, CHANNELS], BF16)
                nc.sync.dma_start(out=x_sb[:], in_=x_rows)

        bias_ps = turn_pool.tile([P, P], BF16, tag="turn")
        nc.tensor.transpose(bias_ps[:], bias_rows[:], ident_bf[:])
        bias_col = keep.tile([P, OUT_TILES], F32)
        nc.vector.tensor_copy(out=bias_col[:], in_=bias_ps[:, 0:OUT_TILES])
        final = n_rounds - 1
        quantise_basis(final - 1, both)
        quantise_weights(final)
        for a in both:
            one = range(a, a + 1)
            exponentials_of_tensor(final, a)
            if a == 0:
                exponents_on_tensor(final, 1)
                multiply(final - 1, range(OUT_TILES), both)
            exponentials_of_squares(final, one)
            quantise_basis(final, one)
            multiply(final, range(OUT_TILES), one)

        for m in range(OUT_TILES):
            res = res_pool.tile([P, 2, CHANNELS], F32)
            nc.vector.scalar_tensor_tensor(
                out=res[:],
                in0=y_ps[m][:].rearrange("r (b c) -> r b c", b=2),
                scalar=bias_col[:, m : m + 1],
                in1=x_sb[:, m : 2 * OUT_TILES : OUT_TILES, :],
                op0=ALU.add,
                op1=ALU.add,
            )
            nc.sync.dma_start(out=out_tiles[:, m : 2 * OUT_TILES : OUT_TILES, :], in_=res[:])
